import numpy as np
import ml_dtypes


def mxq(x, axis, fmt="e4m3"):
    dtype, down = {"e4m3": (ml_dtypes.float8_e4m3fn, 7), "e5m2": (ml_dtypes.float8_e5m2, 14)}[fmt]
    v = np.moveaxis(np.asarray(x, np.float32).astype(ml_dtypes.bfloat16).astype(np.float64), axis, -1)
    blocks = v.reshape(v.shape[:-1] + (-1, 32))
    amax = np.abs(blocks).max(-1, keepdims=True)
    byte = np.maximum(np.where(amax > 0, np.frexp(amax)[1] - 1 + 127, 0) - down, 1)
    scale = np.exp2(byte - 127.0)
    codes = (blocks / scale).astype(np.float32).astype(dtype).astype(np.float64)
    return np.moveaxis((codes * scale).reshape(v.shape), -1, axis)


WIDE = False


def mx_kscale(k):
    if not WIDE:
        return np.ones(k)
    levels = np.array([10, -10, 5, -5, 0])
    a = np.random.permutation(np.resize(levels, k // 512 * 4)).reshape(k // 512, 4)
    idx = np.arange(k)
    return np.exp2(a[idx // 512, idx % 128 // 32])


BF16 = ml_dtypes.bfloat16


def bf(x):
    return np.asarray(x, np.float32).astype(BF16)


def f64(x):
    return np.asarray(x).astype(np.float64)


B, H, T, N, D, GRID = 4, 4, 512, 512, 256, 32


def rot_pairs(v):
    return np.stack((-v[..., 1::2], v[..., ::2]), axis=-1).reshape(v.shape)


def rope(v, c, s):
    return v * c + rot_pairs(v) * s


def setup_inputs():
    s = np.repeat(mx_kscale(N)[::2], 2)
    t = mx_kscale(T)
    u = np.random.random((T, N))
    return {"Q": bf(np.random.standard_normal((B, H, T, N)) * s),
            "K": bf(np.random.standard_normal((B, H, T, N)) * t[:, None] / s),
            "V": bf(np.random.standard_normal((B, 1, T, D)) * 2.0 / np.sqrt(T) / t[:, None]),
            "cos_t": bf(np.cos(2.0 * np.pi * u)),
            "sin_t": bf(np.sin(2.0 * np.pi * u))}


def reference(Q, K, V, cos_t, sin_t):
    c, s = f64(cos_t), f64(sin_t)
    qr = rope(f64(Q), c, s)
    kr = rope(f64(K), c, s)
    scores = (mxq(qr, 3, "e4m3") @ mxq(kr, 3, "e4m3").transpose(0, 1, 3, 2)) / np.sqrt(N)
    return mxq(scores, 3, "e4m3") @ mxq(f64(V), 2, "e4m3")

@@ -1,0 +1,164 @@
+from contextlib import ExitStack
+import math
+
+import concourse.bass as bass
+import concourse.mybir as mybir
+import concourse.tile as tile
+from concourse.masks import make_identity
+
+F32 = mybir.dt.float32
+BF16 = mybir.dt.bfloat16
+U32 = mybir.dt.uint32
+U8 = mybir.dt.uint8
+FP8X4 = mybir.dt.float8_e4m3fn_x4
+MULT = mybir.AluOpType.mult
+COPY = mybir.ActivationFunctionType.Copy
+
+B, H, T, N, D = 4, 4, 512, 512, 256
+P = 128
+R = T // P
+I = N // 2
+HEADS = B * H
+FLOPS = HEADS * (2 * T * T * N + 2 * T * T * D)
+AHEAD = 3
+
+
+def tile_bidirectionalattention_pa_t_kernel(tc, Q, K, V, cos_t, sin_t, out):
+    nc = tc.nc
+    inv_sqrt_n = 1.0 / math.sqrt(N)
+    q_dram = Q.rearrange("b h (p r) n -> (b h) p (r n)", r=R)
+    k_dram = K.rearrange("b h (p r) n -> (b h) p (r n)", r=R)
+    v_dram = V.rearrange("b o (p j) d -> p (b o) (j d)", j=R)
+    o_dram = out.rearrange("b h (p r) d -> (b h) p (r d)", r=R)
+
+    with ExitStack() as ctx:
+        ctx.enter_context(tc.manual_schedule())
+        const = ctx.enter_context(tc.tile_pool(name="const", bufs=1))
+        raw = ctx.enter_context(tc.tile_pool(name="raw", bufs=2 * (AHEAD + 1)))
+        prod = ctx.enter_context(tc.tile_pool(name="prod", bufs=3))
+        grp = ctx.enter_context(tc.tile_pool(name="grp", bufs=3))
+        mxp = ctx.enter_context(tc.tile_pool(name="mxp", bufs=2))
+        opool = ctx.enter_context(tc.tile_pool(name="opool", bufs=3))
+        ps_t = ctx.enter_context(tc.psum_pool(name="ps_t", bufs=4))
+        ps_s = ctx.enter_context(tc.psum_pool(name="ps_s", bufs=2))
+        ps_o = ctx.enter_context(tc.psum_pool(name="ps_o", bufs=2))
+
+        ident = const.tile([P, P], F32, name="ident")
+        make_identity(nc, ident[:])
+        cos_sb = const.tile([P, R * N], BF16, name="cos_sb")
+        sin_sb = const.tile([P, R * N], BF16, name="sin_sb")
+        sx = const.tile([P, R, 2, I], BF16, name="sx")
+        v_raw = const.tile([P, B, R * D], BF16, name="v_raw")
+        v_grp = const.tile([P, B, D, R], BF16, name="v_grp", align_bytes=64)
+
+        st = {}
+
+        def load(g):
+            for nm, src in (("q", q_dram), ("k", k_dram)):
+                t = raw.tile([P, R * N], BF16, name="raw_qk")
+                nc.sync.dma_start(out=t[:], in_=src[g])
+                st[(nm, g)] = t
+
+        def planes(t):
+            return t[:].rearrange("p (r i e) -> p r e i", r=R, e=2)
+
+        def rotate(nm, g):
+            x = planes(st[(nm, g)])
+            a = prod.tile([P, R, 2, I], F32, name="prod_a")
+            b = prod.tile([P, R, 2, I], F32, name="prod_b")
+            nc.vector.tensor_tensor(out=a[:], in0=x, in1=planes(cos_sb), op=MULT)
+            for e in range(2):
+                nc.vector.tensor_tensor(out=b[:, :, e, :], in0=x[:, :, 1 - e, :], in1=sx[:, :, e, :], op=MULT)
+            st[(nm + "ab", g)] = (a, b)
+
+        def transposes(nm, g):
+            a, b = st[(nm + "ab", g)]
+            gt = grp.tile([P, R, P, 4], BF16, name="grp_qk", align_bytes=64)
+            for r in range(R):
+                bank = ps_t.tile([P, 4, P], F32, name="bank_t")
+                for j in range(4):
+                    u, e = j // 2, j % 2
+                    cols = slice(u * P, (u + 1) * P)
+                    nc.tensor.matmul(out=bank[:, j, :], lhsT=a[:, r, e, cols], rhs=ident[:], is_transpose=True, start=True, stop=False)
+                    nc.tensor.matmul(out=bank[:, j, :], lhsT=b[:, r, e, cols], rhs=ident[:], is_transpose=True, start=False, stop=True)
+                nc.scalar.copy(out=gt[:, r, :, :], in_=bank[:].rearrange("p j c -> p c j"))
+            st[(nm + "g", g)] = gt
+
+        def quantise(key, width, tagname):
+            gt = st[key]
+            codes = mxp.tile([P, width], U32, name=tagname + "_codes", align_bytes=64)
+            scales = mxp.tile([P, width], U8, name=tagname + "_scales", align_bytes=64)
+            nc.vector.quantize_mx(out=codes[:].bitcast(FP8X4), scales=scales[:], in_=gt[:].rearrange("p a c j -> p (a c j)"))
+            return codes, scales
+
+        def scores(g):
+            qc, qs = st[("qx", g)]
+            kc, ks = st[("kx", g)]
+            sg = grp.tile([P, R, P, 4], BF16, name="grp_s", align_bytes=64)
+            for rq in range(R):
+                bank = ps_s.tile([P, R, P], F32, name="bank_s")
+                qcols = slice(rq * P, (rq + 1) * P)
+                for rk in range(R):
+                    kcols = slice(rk * P, (rk + 1) * P)
+                    nc.tensor.matmul_mx(out=bank[:, rk, :], lhsT=kc[:, kcols].bitcast(FP8X4), lhsT_scale=ks[:, kcols],
+                                        rhs=qc[:, qcols].bitcast(FP8X4), rhs_scale=qs[:, qcols], start=True, stop=True)
+                nc.scalar.activation(out=sg[:, rq, :, :], in_=bank[:].rearrange("p k c -> p c k"), func=COPY, scale=inv_sqrt_n)
+            st[("sg", g)] = sg
+
+        def values():
+            for b in range(B):
+                nc.scalar.copy(out=v_grp[:, b, :, :], in_=v_raw[:, b, :].rearrange("p (j d) -> p d j", j=R))
+            st["vg"] = v_grp
+
+        def output(g):
+            sc, ss = st[("sx", g)]
+            vc, vs = st["vx"]
+            vcols = slice((g // H) * D, (g // H + 1) * D)
+            ot = opool.tile([P, R, D], F32, name="o_sb")
+            for half in range(R // 2):
+                bank = ps_o.tile([P, 2, D], F32, name="bank_o")
+                for w in range(2):
+                    cols = slice((2 * half + w) * P, (2 * half + w + 1) * P)
+                    nc.tensor.matmul_mx(out=bank[:, w, :], lhsT=sc[:, cols].bitcast(FP8X4), lhsT_scale=ss[:, cols],
+                                        rhs=vc[:, vcols].bitcast(FP8X4), rhs_scale=vs[:, vcols], start=True, stop=True)
+                nc.scalar.copy(out=ot[:, 2 * half:2 * half + 2, :], in_=bank[:])
+            nc.sync.dma_start(out=o_dram[g], in_=ot[:].rearrange("p r d -> p (r d)"))
+
+        nc.sync.dma_start(out=cos_sb[:], in_=cos_t.rearrange("(p r) n -> p (r n)", r=R))
+        t0 = raw.tile([P, R * N], BF16, name="raw_qk")
+        nc.sync.dma_start(out=t0[:], in_=q_dram[0])
+        st[("q", 0)] = t0
+        nc.sync.dma_start(out=sin_sb[:], in_=sin_t.rearrange("(p r) n -> p (r n)", r=R))
+        t1 = raw.tile([P, R * N], BF16, name="raw_qk")
+        nc.sync.dma_start(out=t1[:], in_=k_dram[0])
+        st[("k", 0)] = t1
+        nc.sync.dma_start(out=v_raw[:], in_=v_dram)
+        for g in range(1, AHEAD):
+            load(g)
+        sin_pl = planes(sin_sb)
+        nc.scalar.mul(out=sx[:, :, 0, :], in_=sin_pl[:, :, 0, :], mul=-1.0)
+        nc.scalar.copy(out=sx[:, :, 1, :], in_=sin_pl[:, :, 1, :])
+        values()
+
+        for i in range(HEADS + 2):
+            if i + AHEAD < HEADS:
+                load(i + AHEAD)
+            if i < HEADS:
+                rotate("q", i)
+            if 0 <= i - 1 < HEADS:
+                st[("kx", i - 1)] = quantise(("kg", i - 1), T, "k")
+            if 0 <= i - 2:
+                st[("sx", i - 2)] = quantise(("sg", i - 2), T, "s")
+            if i < HEADS:
+                transposes("q", i)
+            if 0 <= i - 2:
+                output(i - 2)
+            if 0 <= i - 1 < HEADS:
+                scores(i - 1)
+            if i < HEADS:
+                rotate("k", i)
+            if i == 0:
+                st["vx"] = quantise("vg", B * D, "v")
+            if i < HEADS:
+                st[("qx", i)] = quantise(("qg", i), T, "q")
+                transposes("k", i)

@@ -1,9 +1,7 @@
 from contextlib import ExitStack
 import math
 
-import concourse.bass as bass
 import concourse.mybir as mybir
-import concourse.tile as tile
 from concourse.masks import make_identity
 
 F32 = mybir.dt.float32
@@ -21,68 +19,109 @@ I = N // 2
 HEADS = B * H
 FLOPS = HEADS * (2 * T * T * N + 2 * T * T * D)
 AHEAD = 3
+R_POOL = 3
+WARM = True
+TAIL_HELP = False
+PE_ORDER = (("s", 0), ("s", 1), ("s", 2), ("k", 3), ("k", 0), ("s", 3), ("k", 1), ("k", 2),
+            ("o", 0), ("q", 0), ("q", 1), ("o", 1), ("q", 2), ("q", 3))
+
+PE_TAIL = (("k", 3), ("k", 0), ("s", 0), ("s", 1), ("k", 1), ("k", 2), ("s", 2), ("s", 3), ("o", 0), ("o", 1))
 
 
 def tile_bidirectionalattention_pa_t_kernel(tc, Q, K, V, cos_t, sin_t, out):
     nc = tc.nc
     inv_sqrt_n = 1.0 / math.sqrt(N)
-    q_dram = Q.rearrange("b h (p r) n -> (b h) p (r n)", r=R)
-    k_dram = K.rearrange("b h (p r) n -> (b h) p (r n)", r=R)
+    dram = {"q": Q.rearrange("b h (p r) n -> (b h) p (r n)", r=R), "k": K.rearrange("b h (p r) n -> (b h) p (r n)", r=R)}
+    tab_dram = {"c": cos_t.rearrange("(p r) n -> p (r n)", r=R), "s": sin_t.rearrange("(p r) n -> p (r n)", r=R)}
     v_dram = V.rearrange("b o (p j) d -> p (b o) (j d)", j=R)
     o_dram = out.rearrange("b h (p r) d -> (b h) p (r d)", r=R)
+    HALF = R * N // 2
 
     with ExitStack() as ctx:
         ctx.enter_context(tc.manual_schedule())
         const = ctx.enter_context(tc.tile_pool(name="const", bufs=1))
         raw = ctx.enter_context(tc.tile_pool(name="raw", bufs=2 * (AHEAD + 1)))
-        prod = ctx.enter_context(tc.tile_pool(name="prod", bufs=3))
+        prod_v = ctx.enter_context(tc.tile_pool(name="prod_v", bufs=10))
+        prod_g = ctx.enter_context(tc.tile_pool(name="prod_g", bufs=4))
         grp = ctx.enter_context(tc.tile_pool(name="grp", bufs=3))
         mxp = ctx.enter_context(tc.tile_pool(name="mxp", bufs=2))
         opool = ctx.enter_context(tc.tile_pool(name="opool", bufs=3))
-        ps_t = ctx.enter_context(tc.psum_pool(name="ps_t", bufs=4))
-        ps_s = ctx.enter_context(tc.psum_pool(name="ps_s", bufs=2))
-        ps_o = ctx.enter_context(tc.psum_pool(name="ps_o", bufs=2))
+        ps_tab = ctx.enter_context(tc.psum_pool(name="ps_tab", bufs=1))
+        ps = ctx.enter_context(tc.psum_pool(name="ps", bufs=5))
 
         ident = const.tile([P, P], F32, name="ident")
         make_identity(nc, ident[:])
-        cos_sb = const.tile([P, R * N], BF16, name="cos_sb")
-        sin_sb = const.tile([P, R * N], BF16, name="sin_sb")
-        sx = const.tile([P, R, 2, I], BF16, name="sx")
+        ident_bf = const.tile([P, P], BF16, name="ident_bf")
+        make_identity(nc, ident_bf[:])
         v_raw = const.tile([P, B, R * D], BF16, name="v_raw")
         v_grp = const.tile([P, B, D, R], BF16, name="v_grp", align_bytes=64)
-
+        tab_raw = {}
+        tabs = {}
+        tab_ps = {}
         st = {}
 
-        def load(g):
-            for nm, src in (("q", q_dram), ("k", k_dram)):
-                t = raw.tile([P, R * N], BF16, name="raw_qk")
-                nc.sync.dma_start(out=t[:], in_=src[g])
-                st[(nm, g)] = t
+        def load(nm, g, pieces=1):
+            t = raw.tile([P, R * N], BF16, name="raw_qk")
+            w = R * N // pieces
+            for c in range(pieces):
+                nc.sync.dma_start(out=t[:, c * w:(c + 1) * w], in_=dram[nm][g][:, c * w:(c + 1) * w])
+            st[(nm, g)] = t
 
-        def planes(t):
-            return t[:].rearrange("p (r i e) -> p r e i", r=R, e=2)
+        def load_tables(h):
+            for nm in ("c", "s"):
+                t = const.tile([P, HALF], BF16, name="raw_%s%d" % (nm, h))
+                nc.sync.dma_start(out=t[:], in_=tab_dram[nm][:, h * HALF:(h + 1) * HALF])
+                tab_raw[(nm, h)] = t[:].rearrange("p (r i e) -> p r e i", r=2, e=2)
 
-        def rotate(nm, g):
-            x = planes(st[(nm, g)])
-            a = prod.tile([P, R, 2, I], F32, name="prod_a")
-            b = prod.tile([P, R, 2, I], F32, name="prod_b")
-            nc.vector.tensor_tensor(out=a[:], in0=x, in1=planes(cos_sb), op=MULT)
-            for e in range(2):
-                nc.vector.tensor_tensor(out=b[:, :, e, :], in0=x[:, :, 1 - e, :], in1=sx[:, :, e, :], op=MULT)
-            st[(nm + "ab", g)] = (a, b)
+        def prepare_tables(h, eng_cos):
+            t = const.tile([P, 2, 2, 2, I], BF16, name="tabs%d" % h)
+            eng_cos(out=t[:, :, 0, :, :], in_=tab_raw[("c", h)])
+            nc.scalar.copy(out=t[:, :, 1, 0, :], in_=tab_raw[("s", h)][:, :, 1, :])
+            nc.scalar.mul(out=t[:, :, 1, 1, :], in_=tab_raw[("s", h)][:, :, 0, :], mul=-1.0)
+            tabs[h] = t
 
-        def transposes(nm, g):
-            a, b = st[(nm + "ab", g)]
-            gt = grp.tile([P, R, P, 4], BF16, name="grp_qk", align_bytes=64)
-            for r in range(R):
-                bank = ps_t.tile([P, 4, P], F32, name="bank_t")
-                for j in range(4):
-                    u, e = j // 2, j % 2
-                    cols = slice(u * P, (u + 1) * P)
-                    nc.tensor.matmul(out=bank[:, j, :], lhsT=a[:, r, e, cols], rhs=ident[:], is_transpose=True, start=True, stop=False)
-                    nc.tensor.matmul(out=bank[:, j, :], lhsT=b[:, r, e, cols], rhs=ident[:], is_transpose=True, start=False, stop=True)
-                nc.scalar.copy(out=gt[:, r, :, :], in_=bank[:].rearrange("p j c -> p c j"))
-            st[(nm + "g", g)] = gt
+        def table_sb(r):
+            return tabs[r // 2][:, r % 2, :, :, :]
+
+        def table_to_psum(r):
+            tab_ps[r] = ps_tab.tile([P, 2, 2, I], BF16, name="tab_ps%d" % r)
+            for t in range(2):
+                nc.tensor.matmul(out=tab_ps[r][:, t, :, :].rearrange("p e i -> p (e i)"), lhsT=ident_bf[:],
+                                 rhs=table_sb(r)[:, t, :, :].rearrange("p e i -> p (e i)"), start=True, stop=True)
+
+        def products(nm, g, r, from_sbuf=False):
+            x = st[(nm, g)][:].rearrange("p (r i e) -> p r e i", r=R, e=2)[:, r, :, :].unsqueeze(1).to_broadcast([P, 2, 2, I])
+            if r == R_POOL:
+                ab = prod_g.tile([P, 2, 2, I], F32, name="ab_g")
+                nc.gpsimd.tensor_tensor(out=ab[:], in0=x, in1=table_sb(r), op=MULT)
+            else:
+                ab = prod_v.tile([P, 2, 2, I], F32, name="ab_v")
+                nc.vector.tensor_tensor(out=ab[:], in0=x, in1=table_sb(r) if from_sbuf else tab_ps[r][:], op=MULT)
+            st[(nm, g, r)] = ab
+
+        def new_group(nm, g):
+            st[(nm + "g", g)] = grp.tile([P, R, P, 4], BF16, name="grp_" + nm, align_bytes=64)
+
+        def leave_psum(dst, src, scale, on_vector):
+            if on_vector:
+                if scale is None:
+                    nc.vector.tensor_copy(out=dst, in_=src)
+                else:
+                    nc.vector.tensor_scalar(out=dst, in0=src, scalar1=scale, scalar2=None, op0=MULT)
+            elif scale is None:
+                nc.scalar.copy(out=dst, in_=src)
+            else:
+                nc.scalar.activation(out=dst, in_=src, func=COPY, scale=scale)
+
+        def transposes(nm, g, r, on_vector=False):
+            ab = st[(nm, g, r)]
+            bank = ps.tile([P, 4, P], F32, name="bank")
+            for j in range(4):
+                u, e = j // 2, j % 2
+                cols = slice(u * P, (u + 1) * P)
+                nc.tensor.matmul(out=bank[:, j, :], lhsT=ab[:, 0, e, cols], rhs=ident[:], is_transpose=True, start=True, stop=False)
+                nc.tensor.matmul(out=bank[:, j, :], lhsT=ab[:, 1, 1 - e, cols], rhs=ident[:], is_transpose=True, start=False, stop=True)
+            leave_psum(st[(nm + "g", g)][:, r, :, :], bank[:].rearrange("p j c -> p c j"), None, on_vector)
 
         def quantise(key, width, tagname):
             gt = st[key]
@@ -91,74 +130,100 @@ def tile_bidirectionalattention_pa_t_kernel(tc, Q, K, V, cos_t, sin_t, out):
             nc.vector.quantize_mx(out=codes[:].bitcast(FP8X4), scales=scales[:], in_=gt[:].rearrange("p a c j -> p (a c j)"))
             return codes, scales
 
-        def scores(g):
+        def scores(g, rq, on_vector=False):
             qc, qs = st[("qx", g)]
             kc, ks = st[("kx", g)]
-            sg = grp.tile([P, R, P, 4], BF16, name="grp_s", align_bytes=64)
-            for rq in range(R):
-                bank = ps_s.tile([P, R, P], F32, name="bank_s")
-                qcols = slice(rq * P, (rq + 1) * P)
-                for rk in range(R):
-                    kcols = slice(rk * P, (rk + 1) * P)
-                    nc.tensor.matmul_mx(out=bank[:, rk, :], lhsT=kc[:, kcols].bitcast(FP8X4), lhsT_scale=ks[:, kcols],
-                                        rhs=qc[:, qcols].bitcast(FP8X4), rhs_scale=qs[:, qcols], start=True, stop=True)
-                nc.scalar.activation(out=sg[:, rq, :, :], in_=bank[:].rearrange("p k c -> p c k"), func=COPY, scale=inv_sqrt_n)
-            st[("sg", g)] = sg
+            bank = ps.tile([P, R, P], F32, name="bank")
+            qcols = slice(rq * P, (rq + 1) * P)
+            for rk in range(R):
+                kcols = slice(rk * P, (rk + 1) * P)
+                nc.tensor.matmul_mx(out=bank[:, rk, :], lhsT=kc[:, kcols].bitcast(FP8X4), lhsT_scale=ks[:, kcols],
+                                    rhs=qc[:, qcols].bitcast(FP8X4), rhs_scale=qs[:, qcols], start=True, stop=True)
+            leave_psum(st[("sg", g)][:, rq, :, :], bank[:].rearrange("p k c -> p c k"), inv_sqrt_n, on_vector)
 
-        def values():
-            for b in range(B):
-                nc.scalar.copy(out=v_grp[:, b, :, :], in_=v_raw[:, b, :].rearrange("p (j d) -> p d j", j=R))
-            st["vg"] = v_grp
-
-        def output(g):
+        def output(g, half, on_vector=False):
             sc, ss = st[("sx", g)]
             vc, vs = st["vx"]
             vcols = slice((g // H) * D, (g // H + 1) * D)
-            ot = opool.tile([P, R, D], F32, name="o_sb")
-            for half in range(R // 2):
-                bank = ps_o.tile([P, 2, D], F32, name="bank_o")
-                for w in range(2):
-                    cols = slice((2 * half + w) * P, (2 * half + w + 1) * P)
-                    nc.tensor.matmul_mx(out=bank[:, w, :], lhsT=sc[:, cols].bitcast(FP8X4), lhsT_scale=ss[:, cols],
-                                        rhs=vc[:, vcols].bitcast(FP8X4), rhs_scale=vs[:, vcols], start=True, stop=True)
-                nc.scalar.copy(out=ot[:, 2 * half:2 * half + 2, :], in_=bank[:])
-            nc.sync.dma_start(out=o_dram[g], in_=ot[:].rearrange("p r d -> p (r d)"))
+            if half == 0:
+                st[("o", g)] = opool.tile([P, R, D], F32, name="o_sb")
+            ot = st[("o", g)]
+            bank = ps.tile([P, 2, D], F32, name="bank")
+            for w in range(2):
+                cols = slice((2 * half + w) * P, (2 * half + w + 1) * P)
+                nc.tensor.matmul_mx(out=bank[:, w, :], lhsT=sc[:, cols].bitcast(FP8X4), lhsT_scale=ss[:, cols],
+                                    rhs=vc[:, vcols].bitcast(FP8X4), rhs_scale=vs[:, vcols], start=True, stop=True)
+            leave_psum(ot[:, 2 * half:2 * half + 2, :], bank[:], None, on_vector)
+            if half == 1:
+                nc.sync.dma_start(out=o_dram[g], in_=ot[:].rearrange("p r d -> p (r d)"))
 
-        nc.sync.dma_start(out=cos_sb[:], in_=cos_t.rearrange("(p r) n -> p (r n)", r=R))
+        def warm():
+            wb = ps.tile([P, 512], F32, name="bank")
+            nc.tensor.matmul(out=wb[:], lhsT=ident_bf[:], rhs=table_sb(0)[:, 0, :, :].rearrange("p e i -> p (e i)"), start=True, stop=True)
+
+        load_tables(0)
         t0 = raw.tile([P, R * N], BF16, name="raw_qk")
-        nc.sync.dma_start(out=t0[:], in_=q_dram[0])
         st[("q", 0)] = t0
-        nc.sync.dma_start(out=sin_sb[:], in_=sin_t.rearrange("(p r) n -> p (r n)", r=R))
-        t1 = raw.tile([P, R * N], BF16, name="raw_qk")
-        nc.sync.dma_start(out=t1[:], in_=k_dram[0])
-        st[("k", 0)] = t1
+        nc.sync.dma_start(out=t0[:, 0:HALF], in_=dram["q"][0][:, 0:HALF])
+        load_tables(1)
+        nc.sync.dma_start(out=t0[:, HALF:2 * HALF], in_=dram["q"][0][:, HALF:2 * HALF])
+        load("k", 0)
         nc.sync.dma_start(out=v_raw[:], in_=v_dram)
         for g in range(1, AHEAD):
-            load(g)
-        sin_pl = planes(sin_sb)
-        nc.scalar.mul(out=sx[:, :, 0, :], in_=sin_pl[:, :, 0, :], mul=-1.0)
-        nc.scalar.copy(out=sx[:, :, 1, :], in_=sin_pl[:, :, 1, :])
-        values()
+            load("q", g)
+            load("k", g)
+        prepare_tables(0, nc.vector.tensor_copy)
+        table_to_psum(0)
+        table_to_psum(1)
+        prepare_tables(1, nc.scalar.copy)
+        table_to_psum(2)
+        for b in range(B):
+            nc.scalar.copy(out=v_grp[:, b, :, :], in_=v_raw[:, b, :].rearrange("p (j d) -> p d j", j=R))
+        st["vg"] = v_grp
 
-        for i in range(HEADS + 2):
-            if i + AHEAD < HEADS:
-                load(i + AHEAD)
-            if i < HEADS:
-                rotate("q", i)
-            if 0 <= i - 1 < HEADS:
-                st[("kx", i - 1)] = quantise(("kg", i - 1), T, "k")
-            if 0 <= i - 2:
-                st[("sx", i - 2)] = quantise(("sg", i - 2), T, "s")
-            if i < HEADS:
-                transposes("q", i)
-            if 0 <= i - 2:
-                output(i - 2)
-            if 0 <= i - 1 < HEADS:
-                scores(i - 1)
-            if i < HEADS:
-                rotate("k", i)
-            if i == 0:
+        for j in range(HEADS + 4):
+            rot, trk, sco, fin = j < HEADS, 0 <= j - 1 < HEADS, 0 <= j - 2 < HEADS, 0 <= j - 3 < HEADS
+            if j + AHEAD < HEADS:
+                load("q", j + AHEAD)
+                load("k", j + AHEAD)
+            if rot:
+                products("q", j, R_POOL)
+                products("k", j, R_POOL)
+                for r in range(3):
+                    products("q", j, r, from_sbuf=(j == 0 and r < 2))
+                new_group("q", j)
+            if sco:
+                new_group("s", j - 2)
+            if trk:
+                new_group("k", j - 1)
+            tail = TAIL_HELP and j >= HEADS
+            turn = 0
+            for step in (PE_TAIL if tail else PE_ORDER):
+                turn += 1
+                helper = tail and turn % 2 == 0
+                if step[0] == "s":
+                    if sco:
+                        scores(j - 2, step[1], helper)
+                    elif WARM and j < 2:
+                        warm()
+                if step[0] == "o":
+                    if fin:
+                        output(j - 3, step[1], helper)
+                    elif WARM and j < 3:
+                        warm()
+                if step[0] == "k" and trk:
+                    transposes("k", j - 1, step[1], helper)
+                if step[0] == "q" and rot:
+                    transposes("q", j, step[1])
+            if rot:
+                for r in range(3):
+                    products("k", j, r)
+            if j == 0:
                 st["vx"] = quantise("vg", B * D, "v")
-            if i < HEADS:
-                st[("qx", i)] = quantise(("qg", i), T, "q")
-                transposes("k", i)
+            if sco and not tail:
+                st[("sx", j - 2)] = quantise(("sg", j - 2), T, "s")
+            if trk:
+                st[("qx", j - 1)] = quantise(("qg", j - 1), T, "q")
+                st[("kx", j - 1)] = quantise(("kg", j - 1), T, "k")
+            if sco and tail:
+                st[("sx", j - 2)] = quantise(("sg", j - 2), T, "s")

@@ -21,6 +21,7 @@ FLOPS = HEADS * (2 * T * T * N + 2 * T * T * D)
 AHEAD = 3
 R_POOL = 3
 WARM = True
+SHARED = ("k", 2)
 TAIL_HELP = False
 PE_ORDER = (("s", 0), ("s", 1), ("s", 2), ("k", 3), ("k", 0), ("s", 3), ("k", 1), ("k", 2),
             ("o", 0), ("q", 0), ("q", 1), ("o", 1), ("q", 2), ("q", 3))
@@ -89,7 +90,18 @@ def tile_bidirectionalattention_pa_t_kernel(tc, Q, K, V, cos_t, sin_t, out):
                 nc.tensor.matmul(out=tab_ps[r][:, t, :, :].rearrange("p e i -> p (e i)"), lhsT=ident_bf[:],
                                  rhs=table_sb(r)[:, t, :, :].rearrange("p e i -> p (e i)"), start=True, stop=True)
 
+        def shared_products(nm, g, r, on_pool):
+            x = st[(nm, g)][:].rearrange("p (r i e) -> p r e i", r=R, e=2)[:, r, :, :]
+            if on_pool:
+                st[(nm, g, r)] = prod_v.tile([P, 2, 2, I], F32, name="ab_s", bufs=3)
+                nc.gpsimd.tensor_tensor(out=st[(nm, g, r)][:, 1, :, :], in0=x, in1=table_sb(r)[:, 1, :, :], op=MULT)
+            else:
+                nc.vector.tensor_tensor(out=st[(nm, g, r)][:, 0, :, :], in0=x, in1=tab_ps[r][:, 0, :, :], op=MULT)
+
         def products(nm, g, r, from_sbuf=False):
+            if (nm, r) == SHARED:
+                shared_products(nm, g, r, False)
+                return
             x = st[(nm, g)][:].rearrange("p (r i e) -> p r e i", r=R, e=2)[:, r, :, :].unsqueeze(1).to_broadcast([P, 2, 2, I])
             if r == R_POOL:
                 ab = prod_g.tile([P, 2, 2, I], F32, name="ab_g")
@@ -189,6 +201,8 @@ def tile_bidirectionalattention_pa_t_kernel(tc, Q, K, V, cos_t, sin_t, out):
             if rot:
                 products("q", j, R_POOL)
                 products("k", j, R_POOL)
+                if SHARED is not None:
+                    shared_products(SHARED[0], j, SHARED[1], True)
                 for r in range(3):
                     products("q", j, r, from_sbuf=(j == 0 and r < 2))
                 new_group("q", j)

@@ -21,6 +21,8 @@ FLOPS = HEADS * (2 * T * T * N + 2 * T * T * D)
 AHEAD = 3
 R_POOL = 3
 WARM = True
+V_TAKES_ODD = ()
+V_TAKES = (("o", 1),)
 SHARED = ("k", 2)
 TAIL_HELP = False
 PE_ORDER = (("s", 0), ("s", 1), ("s", 2), ("k", 3), ("k", 0), ("s", 3), ("k", 1), ("k", 2),
@@ -114,8 +116,13 @@ def tile_bidirectionalattention_pa_t_kernel(tc, Q, K, V, cos_t, sin_t, out):
         def new_group(nm, g):
             st[(nm + "g", g)] = grp.tile([P, R, P, 4], BF16, name="grp_" + nm, align_bytes=64)
 
+        st["deferred"] = []
+        st["stores"] = []
+
         def leave_psum(dst, src, scale, on_vector):
-            if on_vector:
+            if on_vector == "later":
+                st["deferred"].append((dst, src, scale))
+            elif on_vector:
                 if scale is None:
                     nc.vector.tensor_copy(out=dst, in_=src)
                 else:
@@ -167,7 +174,18 @@ def tile_bidirectionalattention_pa_t_kernel(tc, Q, K, V, cos_t, sin_t, out):
                                     rhs=vc[:, vcols].bitcast(FP8X4), rhs_scale=vs[:, vcols], start=True, stop=True)
             leave_psum(ot[:, 2 * half:2 * half + 2, :], bank[:], None, on_vector)
             if half == 1:
+                if st["deferred"]:
+                    st["stores"].append((g, ot))
+                else:
+                    nc.sync.dma_start(out=o_dram[g], in_=ot[:].rearrange("p r d -> p (r d)"))
+
+        def flush_deferred():
+            for dst, src, scale in st["deferred"]:
+                leave_psum(dst, src, scale, True)
+            for g, ot in st["stores"]:
                 nc.sync.dma_start(out=o_dram[g], in_=ot[:].rearrange("p r d -> p (r d)"))
+            st["deferred"] = []
+            st["stores"] = []
 
         def warm():
             wb = ps.tile([P, 512], F32, name="bank")
@@ -214,7 +232,7 @@ def tile_bidirectionalattention_pa_t_kernel(tc, Q, K, V, cos_t, sin_t, out):
             turn = 0
             for step in (PE_TAIL if tail else PE_ORDER):
                 turn += 1
-                helper = tail and turn % 2 == 0
+                helper = "later" if (step in V_TAKES or (j % 2 == 1 and step in V_TAKES_ODD)) else False
                 if step[0] == "s":
                     if sco:
                         scores(j - 2, step[1], helper)
@@ -228,7 +246,7 @@ def tile_bidirectionalattention_pa_t_kernel(tc, Q, K, V, cos_t, sin_t, out):
                 if step[0] == "k" and trk:
                     transposes("k", j - 1, step[1], helper)
                 if step[0] == "q" and rot:
-                    transposes("q", j, step[1])
+                    transposes("q", j, step[1], helper)
             if rot:
                 for r in range(3):
                     products("k", j, r)
@@ -241,3 +259,4 @@ def tile_bidirectionalattention_pa_t_kernel(tc, Q, K, V, cos_t, sin_t, out):
                 st[("kx", j - 1)] = quantise(("kg", j - 1), T, "k")
             if sco and tail:
                 st[("sx", j - 2)] = quantise(("sg", j - 2), T, "s")
+            flush_deferred()

@@ -17,18 +17,40 @@ P = 128
 R = T // P
 I = N // 2
 HEADS = B * H
+LAST = HEADS - 1
 FLOPS = HEADS * (2 * T * T * N + 2 * T * T * D)
 AHEAD = 3
 R_POOL = 3
-WARM = True
-V_TAKES_ODD = ()
-V_TAKES = (("o", 1),)
 SHARED = ("k", 2)
-TAIL_HELP = False
-PE_ORDER = (("s", 0), ("s", 1), ("s", 2), ("k", 3), ("k", 0), ("s", 3), ("k", 1), ("k", 2),
-            ("o", 0), ("q", 0), ("q", 1), ("o", 1), ("q", 2), ("q", 3))
-
-PE_TAIL = (("k", 3), ("k", 0), ("s", 0), ("s", 1), ("k", 1), ("k", 2), ("s", 2), ("s", 3), ("o", 0), ("o", 1))
+WARM = True
+SHARE_FROM = 1
+POOL_PREP = False
+EARLY_ORDER = True
+BURST_DUMMY = False
+PE_ORDER = (("s", 0, 2), ("s", 1, 2), ("s", 2, 2), ("k", 3, 1), ("k", 0, 1), ("s", 3, 2), ("k", 1, 1), ("k", 2, 1),
+            ("o", 0, 3), ("q", 0, 0), ("q", 1, 0), ("o", 1, 3), ("q", 2, 0), ("q", 3, 0))
+PE_LAST = (("s", 0, 2), ("s", 1, 2), ("s", 2, 2), ("k", 3, 1), ("k", 0, 1), ("s", 3, 2), ("k", 1, 1), ("k", 2, 1),
+           ("o", 0, 3), ("k", 3, 0), ("k", 0, 0), ("o", 1, 3), ("k", 1, 0), ("k", 2, 0))
+SC, VE = "scalar", "vector"
+EPILOGUE = (
+    ("Z", "s", LAST - 2), ("Z", "q", LAST - 1), ("Z", "k", LAST - 1),
+    ("T", "q", 3, SC), ("T", "q", 0, SC),
+    ("Z", "k", LAST),
+    ("S", LAST - 1, 0, SC), ("S", LAST - 1, 1, VE),
+    ("ZS", "q", 3), ("ZS", "q", 0),
+    ("T", "q", 1, SC), ("T", "q", 2, SC),
+    ("S", LAST, 3, VE), ("S", LAST, 0, SC),
+    ("ZS", "q", 1), ("ZS", "q", 2),
+    ("S", LAST - 1, 2, SC), ("S", LAST - 1, 3, VE),
+    ("ZS", "s", 3), ("ZS", "s", 0),
+    ("S", LAST, 1, SC), ("S", LAST, 2, VE),
+    ("O", LAST - 2, 0, SC), ("O", LAST - 2, 1, SC),
+    ("Z", "s", LAST - 1),
+    ("OS", 3, SC), ("OS", 0, SC),
+    ("ZS", "s", 1), ("ZS", "s", 2),
+    ("O", LAST - 1, 0, VE), ("O", LAST - 1, 1, SC),
+    ("OS", 1, VE), ("OS", 2, SC),
+)
 
 
 def tile_bidirectionalattention_pa_t_kernel(tc, Q, K, V, cos_t, sin_t, out):
@@ -58,16 +80,16 @@ def tile_bidirectionalattention_pa_t_kernel(tc, Q, K, V, cos_t, sin_t, out):
         make_identity(nc, ident_bf[:])
         v_raw = const.tile([P, B, R * D], BF16, name="v_raw")
         v_grp = const.tile([P, B, D, R], BF16, name="v_grp", align_bytes=64)
+        v_codes = const.tile([P, B * D], U32, name="v_codes", align_bytes=64)
+        v_scales = const.tile([P, B * D], U8, name="v_scales", align_bytes=64)
         tab_raw = {}
         tabs = {}
         tab_ps = {}
         st = {}
 
-        def load(nm, g, pieces=1):
+        def load(nm, g):
             t = raw.tile([P, R * N], BF16, name="raw_qk")
-            w = R * N // pieces
-            for c in range(pieces):
-                nc.sync.dma_start(out=t[:, c * w:(c + 1) * w], in_=dram[nm][g][:, c * w:(c + 1) * w])
+            nc.sync.dma_start(out=t[:], in_=dram[nm][g])
             st[(nm, g)] = t
 
         def load_tables(h):
@@ -83,6 +105,9 @@ def tile_bidirectionalattention_pa_t_kernel(tc, Q, K, V, cos_t, sin_t, out):
             nc.scalar.mul(out=t[:, :, 1, 1, :], in_=tab_raw[("s", h)][:, :, 0, :], mul=-1.0)
             tabs[h] = t
 
+        def pool_copy(out, in_):
+            nc.gpsimd.tensor_scalar(out=out, in0=in_, scalar1=1.0, scalar2=0.0, op0=MULT, op1=mybir.AluOpType.add)
+
         def table_sb(r):
             return tabs[r // 2][:, r % 2, :, :, :]
 
@@ -92,47 +117,44 @@ def tile_bidirectionalattention_pa_t_kernel(tc, Q, K, V, cos_t, sin_t, out):
                 nc.tensor.matmul(out=tab_ps[r][:, t, :, :].rearrange("p e i -> p (e i)"), lhsT=ident_bf[:],
                                  rhs=table_sb(r)[:, t, :, :].rearrange("p e i -> p (e i)"), start=True, stop=True)
 
-        def shared_products(nm, g, r, on_pool):
-            x = st[(nm, g)][:].rearrange("p (r i e) -> p r e i", r=R, e=2)[:, r, :, :]
-            if on_pool:
+        def planes(nm, g, r):
+            return st[(nm, g)][:].rearrange("p (r i e) -> p r e i", r=R, e=2)[:, r, :, :]
+
+        def pool_products(nm, g):
+            ab = prod_g.tile([P, 2, 2, I], F32, name="ab_g")
+            nc.gpsimd.tensor_tensor(out=ab[:], in0=planes(nm, g, R_POOL).unsqueeze(1).to_broadcast([P, 2, 2, I]), in1=table_sb(R_POOL), op=MULT)
+            st[(nm, g, R_POOL)] = ab
+            if nm == SHARED[0] and g >= SHARE_FROM:
+                r = SHARED[1]
                 st[(nm, g, r)] = prod_v.tile([P, 2, 2, I], F32, name="ab_s", bufs=3)
-                nc.gpsimd.tensor_tensor(out=st[(nm, g, r)][:, 1, :, :], in0=x, in1=table_sb(r)[:, 1, :, :], op=MULT)
-            else:
-                nc.vector.tensor_tensor(out=st[(nm, g, r)][:, 0, :, :], in0=x, in1=tab_ps[r][:, 0, :, :], op=MULT)
+                nc.gpsimd.tensor_tensor(out=st[(nm, g, r)][:, 1, :, :], in0=planes(nm, g, r), in1=table_sb(r)[:, 1, :, :], op=MULT)
 
         def products(nm, g, r, from_sbuf=False):
-            if (nm, r) == SHARED:
-                shared_products(nm, g, r, False)
+            if (nm, r) == SHARED and g >= SHARE_FROM:
+                nc.vector.tensor_tensor(out=st[(nm, g, r)][:, 0, :, :], in0=planes(nm, g, r), in1=tab_ps[r][:, 0, :, :], op=MULT)
                 return
-            x = st[(nm, g)][:].rearrange("p (r i e) -> p r e i", r=R, e=2)[:, r, :, :].unsqueeze(1).to_broadcast([P, 2, 2, I])
-            if r == R_POOL:
-                ab = prod_g.tile([P, 2, 2, I], F32, name="ab_g")
-                nc.gpsimd.tensor_tensor(out=ab[:], in0=x, in1=table_sb(r), op=MULT)
-            else:
-                ab = prod_v.tile([P, 2, 2, I], F32, name="ab_v")
-                nc.vector.tensor_tensor(out=ab[:], in0=x, in1=table_sb(r) if from_sbuf else tab_ps[r][:], op=MULT)
+            ab = prod_v.tile([P, 2, 2, I], F32, name="ab_v")
+            nc.vector.tensor_tensor(out=ab[:], in0=planes(nm, g, r).unsqueeze(1).to_broadcast([P, 2, 2, I]),
+                                    in1=table_sb(r) if from_sbuf else tab_ps[r][:], op=MULT)
             st[(nm, g, r)] = ab
 
-        def new_group(nm, g):
-            st[(nm + "g", g)] = grp.tile([P, R, P, 4], BF16, name="grp_" + nm, align_bytes=64)
+        def group_tile(nm, g):
+            if (nm + "g", g) not in st:
+                st[(nm + "g", g)] = grp.tile([P, R, P, 4], BF16, name="grp_" + nm, align_bytes=64)
+            return st[(nm + "g", g)]
 
-        st["deferred"] = []
-        st["stores"] = []
-
-        def leave_psum(dst, src, scale, on_vector):
-            if on_vector == "later":
-                st["deferred"].append((dst, src, scale))
-            elif on_vector:
+        def leave_psum(dst, src, scale, eng):
+            if eng == VE:
                 if scale is None:
                     nc.vector.tensor_copy(out=dst, in_=src)
                 else:
-                    nc.vector.tensor_scalar(out=dst, in0=src, scalar1=scale, scalar2=None, op0=MULT)
+                    nc.vector.tensor_scalar_mul(out=dst, in0=src, scalar1=scale)
             elif scale is None:
                 nc.scalar.copy(out=dst, in_=src)
             else:
                 nc.scalar.activation(out=dst, in_=src, func=COPY, scale=scale)
 
-        def transposes(nm, g, r, on_vector=False):
+        def transposes(nm, g, r, eng=SC):
             ab = st[(nm, g, r)]
             bank = ps.tile([P, 4, P], F32, name="bank")
             for j in range(4):
@@ -140,52 +162,56 @@ def tile_bidirectionalattention_pa_t_kernel(tc, Q, K, V, cos_t, sin_t, out):
                 cols = slice(u * P, (u + 1) * P)
                 nc.tensor.matmul(out=bank[:, j, :], lhsT=ab[:, 0, e, cols], rhs=ident[:], is_transpose=True, start=True, stop=False)
                 nc.tensor.matmul(out=bank[:, j, :], lhsT=ab[:, 1, 1 - e, cols], rhs=ident[:], is_transpose=True, start=False, stop=True)
-            leave_psum(st[(nm + "g", g)][:, r, :, :], bank[:].rearrange("p j c -> p c j"), None, on_vector)
+            leave_psum(group_tile(nm, g)[:, r, :, :], bank[:].rearrange("p j c -> p c j"), None, eng)
 
-        def quantise(key, width, tagname):
-            gt = st[key]
-            codes = mxp.tile([P, width], U32, name=tagname + "_codes", align_bytes=64)
-            scales = mxp.tile([P, width], U8, name=tagname + "_scales", align_bytes=64)
-            nc.vector.quantize_mx(out=codes[:].bitcast(FP8X4), scales=scales[:], in_=gt[:].rearrange("p a c j -> p (a c j)"))
-            return codes, scales
+        def code_tiles(nm, g):
+            if (nm + "x", g) not in st:
+                st[(nm + "x", g)] = (mxp.tile([P, T], U32, name=nm + "_codes", align_bytes=64),
+                                     mxp.tile([P, T], U8, name=nm + "_scales", align_bytes=64))
+            return st[(nm + "x", g)]
 
-        def scores(g, rq, on_vector=False):
-            qc, qs = st[("qx", g)]
-            kc, ks = st[("kx", g)]
+        def quantise(nm, g, r=None):
+            codes, scales = code_tiles(nm, g)
+            gt = group_tile(nm, g)
+            if r is None:
+                nc.vector.quantize_mx(out=codes[:].bitcast(FP8X4), scales=scales[:], in_=gt[:].rearrange("p a c j -> p (a c j)"))
+            else:
+                cols = slice(r * P, (r + 1) * P)
+                nc.vector.quantize_mx(out=codes[:, cols].bitcast(FP8X4), scales=scales[:, cols], in_=gt[:, r, :, :].rearrange("p c j -> p (c j)"))
+
+        def values(b):
+            nc.scalar.copy(out=v_grp[:, b, :, :], in_=v_raw[:, b, :].rearrange("p (j d) -> p d j", j=R))
+
+        def quantise_values(b):
+            cols = slice(b * D, (b + 1) * D)
+            nc.vector.quantize_mx(out=v_codes[:, cols].bitcast(FP8X4), scales=v_scales[:, cols], in_=v_grp[:, b, :, :].rearrange("p d j -> p (d j)"))
+
+        def scores(g, rq, eng=SC):
+            qc, qs = code_tiles("q", g)
+            kc, ks = code_tiles("k", g)
             bank = ps.tile([P, R, P], F32, name="bank")
             qcols = slice(rq * P, (rq + 1) * P)
             for rk in range(R):
                 kcols = slice(rk * P, (rk + 1) * P)
                 nc.tensor.matmul_mx(out=bank[:, rk, :], lhsT=kc[:, kcols].bitcast(FP8X4), lhsT_scale=ks[:, kcols],
                                     rhs=qc[:, qcols].bitcast(FP8X4), rhs_scale=qs[:, qcols], start=True, stop=True)
-            leave_psum(st[("sg", g)][:, rq, :, :], bank[:].rearrange("p k c -> p c k"), inv_sqrt_n, on_vector)
+            leave_psum(group_tile("s", g)[:, rq, :, :], bank[:].rearrange("p k c -> p c k"), inv_sqrt_n, eng)
 
-        def output(g, half, on_vector=False):
-            sc, ss = st[("sx", g)]
-            vc, vs = st["vx"]
+        def output(g, first, count, eng=SC):
+            sc, ss = code_tiles("s", g)
             vcols = slice((g // H) * D, (g // H + 1) * D)
-            if half == 0:
+            if ("o", g) not in st:
                 st[("o", g)] = opool.tile([P, R, D], F32, name="o_sb")
             ot = st[("o", g)]
             bank = ps.tile([P, 2, D], F32, name="bank")
-            for w in range(2):
-                cols = slice((2 * half + w) * P, (2 * half + w + 1) * P)
+            for w in range(count):
+                cols = slice((first + w) * P, (first + w + 1) * P)
                 nc.tensor.matmul_mx(out=bank[:, w, :], lhsT=sc[:, cols].bitcast(FP8X4), lhsT_scale=ss[:, cols],
-                                    rhs=vc[:, vcols].bitcast(FP8X4), rhs_scale=vs[:, vcols], start=True, stop=True)
-            leave_psum(ot[:, 2 * half:2 * half + 2, :], bank[:], None, on_vector)
-            if half == 1:
-                if st["deferred"]:
-                    st["stores"].append((g, ot))
-                else:
-                    nc.sync.dma_start(out=o_dram[g], in_=ot[:].rearrange("p r d -> p (r d)"))
+                                    rhs=v_codes[:, vcols].bitcast(FP8X4), rhs_scale=v_scales[:, vcols], start=True, stop=True)
+            leave_psum(ot[:, first:first + count, :], bank[:, 0:count, :], None, eng)
 
-        def flush_deferred():
-            for dst, src, scale in st["deferred"]:
-                leave_psum(dst, src, scale, True)
-            for g, ot in st["stores"]:
-                nc.sync.dma_start(out=o_dram[g], in_=ot[:].rearrange("p r d -> p (r d)"))
-            st["deferred"] = []
-            st["stores"] = []
+        def store(g, first, count):
+            nc.sync.dma_start(out=o_dram[g][:, first * D:(first + count) * D], in_=st[("o", g)][:, first:first + count, :].rearrange("p r d -> p (r d)"))
 
         def warm():
             wb = ps.tile([P, 512], F32, name="bank")
@@ -198,65 +224,72 @@ def tile_bidirectionalattention_pa_t_kernel(tc, Q, K, V, cos_t, sin_t, out):
         load_tables(1)
         nc.sync.dma_start(out=t0[:, HALF:2 * HALF], in_=dram["q"][0][:, HALF:2 * HALF])
         load("k", 0)
-        nc.sync.dma_start(out=v_raw[:], in_=v_dram)
         for g in range(1, AHEAD):
             load("q", g)
             load("k", g)
+        nc.sync.dma_start(out=v_raw[:], in_=v_dram)
         prepare_tables(0, nc.vector.tensor_copy)
         table_to_psum(0)
         table_to_psum(1)
-        prepare_tables(1, nc.scalar.copy)
+        prepare_tables(1, pool_copy if POOL_PREP else nc.scalar.copy)
         table_to_psum(2)
-        for b in range(B):
-            nc.scalar.copy(out=v_grp[:, b, :, :], in_=v_raw[:, b, :].rearrange("p (j d) -> p d j", j=R))
-        st["vg"] = v_grp
 
-        for j in range(HEADS + 4):
-            rot, trk, sco, fin = j < HEADS, 0 <= j - 1 < HEADS, 0 <= j - 2 < HEADS, 0 <= j - 3 < HEADS
+        for j in range(HEADS):
+            last = j == LAST
             if j + AHEAD < HEADS:
                 load("q", j + AHEAD)
                 load("k", j + AHEAD)
-            if rot:
-                products("q", j, R_POOL)
-                products("k", j, R_POOL)
-                if SHARED is not None:
-                    shared_products(SHARED[0], j, SHARED[1], True)
-                for r in range(3):
-                    products("q", j, r, from_sbuf=(j == 0 and r < 2))
-                new_group("q", j)
-            if sco:
-                new_group("s", j - 2)
-            if trk:
-                new_group("k", j - 1)
-            tail = TAIL_HELP and j >= HEADS
-            turn = 0
-            for step in (PE_TAIL if tail else PE_ORDER):
-                turn += 1
-                helper = "later" if (step in V_TAKES or (j % 2 == 1 and step in V_TAKES_ODD)) else False
-                if step[0] == "s":
-                    if sco:
-                        scores(j - 2, step[1], helper)
-                    elif WARM and j < 2:
+            first_nm, second_nm = ("k", "q") if last else ("q", "k")
+            pool_products(first_nm, j)
+            pool_products(second_nm, j)
+            early = EARLY_ORDER and j == 0
+            for r in range(2 if early else 3):
+                products(first_nm, j, r, from_sbuf=(j == 0 and r < 2))
+            if early:
+                products(second_nm, j, 0)
+                products(second_nm, j, 1)
+                products(first_nm, j, 2)
+            for kind, idx, lag in (PE_LAST if last else PE_ORDER):
+                g = j - lag
+                if g < 0:
+                    if WARM and kind in ("s", "o"):
                         warm()
-                if step[0] == "o":
-                    if fin:
-                        output(j - 3, step[1], helper)
-                    elif WARM and j < 3:
+                elif kind == "s":
+                    scores(g, idx)
+                    if BURST_DUMMY and idx == 0:
                         warm()
-                if step[0] == "k" and trk:
-                    transposes("k", j - 1, step[1], helper)
-                if step[0] == "q" and rot:
-                    transposes("q", j, step[1], helper)
-            if rot:
-                for r in range(3):
-                    products("k", j, r)
-            if j == 0:
-                st["vx"] = quantise("vg", B * D, "v")
-            if sco and not tail:
-                st[("sx", j - 2)] = quantise(("sg", j - 2), T, "s")
-            if trk:
-                st[("qx", j - 1)] = quantise(("qg", j - 1), T, "q")
-                st[("kx", j - 1)] = quantise(("kg", j - 1), T, "k")
-            if sco and tail:
-                st[("sx", j - 2)] = quantise(("sg", j - 2), T, "s")
-            flush_deferred()
+                elif kind == "o":
+                    output(g, 2 * idx, 2)
+                    if idx == 1:
+                        store(g, 0, R)
+                else:
+                    transposes(kind, g, idx)
+            if j < B:
+                values(j)
+            for r in range(2 if early else 0, 3):
+                products(second_nm, j, r)
+            if not last:
+                if j >= 2:
+                    quantise("s", j - 2)
+                if j >= 1:
+                    quantise("q", j - 1)
+                    quantise("k", j - 1)
+                if 1 <= j <= B:
+                    quantise_values(j - 1)
+
+        for step in EPILOGUE:
+            if step[0] == "Z":
+                quantise(step[1], step[2])
+            elif step[0] == "ZS":
+                quantise(step[1], LAST, step[2])
+            elif step[0] == "T":
+                transposes(step[1], LAST, step[2], step[3])
+            elif step[0] == "S":
+                scores(step[1], step[2], step[3])
+            elif step[0] == "O":
+                output(step[1], 2 * step[2], 2, step[3])
+                if step[2] == 1:
+                    store(step[1], 0, R)
+            elif step[0] == "OS":
+                output(LAST, step[1], 1, step[2])
+        store(LAST, 0, R)

@@ -22,7 +22,7 @@ FLOPS = HEADS * (2 * T * T * N + 2 * T * T * D)
 AHEAD = 3
 R_POOL = 3
 SHARED = ("k", 2)
-WARM = True
+WARM = False
 SHARE_FROM = 1
 POOL_PREP = False
 EARLY_ORDER = True

@@ -82,6 +82,7 @@ def tile_bidirectionalattention_pa_t_kernel(tc, Q, K, V, cos_t, sin_t, out):
         v_grp = const.tile([P, B, D, R], BF16, name="v_grp", align_bytes=64)
         v_codes = const.tile([P, B * D], U32, name="v_codes", align_bytes=64)
         v_scales = const.tile([P, B * D], U8, name="v_scales", align_bytes=64)
+        gate = const.tile([P, 1], U32, name="gate")
         tab_raw = {}
         tabs = {}
         tab_ps = {}
@@ -240,6 +241,8 @@ def tile_bidirectionalattention_pa_t_kernel(tc, Q, K, V, cos_t, sin_t, out):
                 load("q", j + AHEAD)
                 load("k", j + AHEAD)
             first_nm, second_nm = ("k", "q") if last else ("q", "k")
+            if j >= 2:
+                nc.gpsimd.tensor_copy(out=gate[:], in_=code_tiles("k", j - 2)[0][:, 0:1])
             pool_products(first_nm, j)
             pool_products(second_nm, j)
             early = EARLY_ORDER and j == 0

@@ -27,10 +27,10 @@ SHARE_FROM = 1
 POOL_PREP = False
 EARLY_ORDER = True
 BURST_DUMMY = False
-PE_ORDER = (("s", 0, 2), ("s", 1, 2), ("s", 2, 2), ("k", 3, 1), ("k", 0, 1), ("s", 3, 2), ("k", 1, 1), ("k", 2, 1),
-            ("o", 0, 3), ("q", 0, 0), ("q", 1, 0), ("o", 1, 3), ("q", 2, 0), ("q", 3, 0))
-PE_LAST = (("s", 0, 2), ("s", 1, 2), ("s", 2, 2), ("k", 3, 1), ("k", 0, 1), ("s", 3, 2), ("k", 1, 1), ("k", 2, 1),
-           ("o", 0, 3), ("k", 3, 0), ("k", 0, 0), ("o", 1, 3), ("k", 1, 0), ("k", 2, 0))
+PE_ORDER = (("s", 0, 2), ("s", 1, 2), ("s", 2, 2), ("s", 3, 2), ("o", 0, 3), ("o", 1, 3), ("k", 3, 1), ("k", 0, 1), ("k", 1, 1), ("k", 2, 1),
+            ("q", 0, 0), ("q", 1, 0), ("q", 2, 0), ("q", 3, 0))
+PE_LAST = (("s", 0, 2), ("s", 1, 2), ("s", 2, 2), ("s", 3, 2), ("o", 0, 3), ("o", 1, 3), ("k", 3, 1), ("k", 0, 1), ("k", 1, 1), ("k", 2, 1),
+           ("k", 3, 0), ("k", 0, 0), ("k", 1, 0), ("k", 2, 0))
 SC, VE = "scalar", "vector"
 EPILOGUE = (
     ("Z", "s", LAST - 2), ("Z", "q", LAST - 1), ("Z", "k", LAST - 1),

@@ -21,36 +21,15 @@ LAST = HEADS - 1
 FLOPS = HEADS * (2 * T * T * N + 2 * T * T * D)
 AHEAD = 3
 R_POOL = 3
-SHARED = ("k", 2)
-WARM = False
-SHARE_FROM = 1
-POOL_PREP = False
-EARLY_ORDER = True
-BURST_DUMMY = False
-PE_ORDER = (("s", 0, 2), ("s", 1, 2), ("s", 2, 2), ("s", 3, 2), ("o", 0, 3), ("o", 1, 3), ("k", 3, 1), ("k", 0, 1), ("k", 1, 1), ("k", 2, 1),
-            ("q", 0, 0), ("q", 1, 0), ("q", 2, 0), ("q", 3, 0))
-PE_LAST = (("s", 0, 2), ("s", 1, 2), ("s", 2, 2), ("s", 3, 2), ("o", 0, 3), ("o", 1, 3), ("k", 3, 1), ("k", 0, 1), ("k", 1, 1), ("k", 2, 1),
-           ("k", 3, 0), ("k", 0, 0), ("k", 1, 0), ("k", 2, 0))
+R_SHARED = 2
+SHARE_FROM = 0
+GATE = True
+TILES = (0, 1, 2, 3)
+SEC_TILES = (3, 0, 1, 2)
+HOLD1 = (256, 0, 256, 0)
+HOLD2 = (0, 0, 256, 0)
+ORDER = ("2", "1", "s", "o")
 SC, VE = "scalar", "vector"
-EPILOGUE = (
-    ("Z", "s", LAST - 2), ("Z", "q", LAST - 1), ("Z", "k", LAST - 1),
-    ("T", "q", 3, SC), ("T", "q", 0, SC),
-    ("Z", "k", LAST),
-    ("S", LAST - 1, 0, SC), ("S", LAST - 1, 1, VE),
-    ("ZS", "q", 3), ("ZS", "q", 0),
-    ("T", "q", 1, SC), ("T", "q", 2, SC),
-    ("S", LAST, 3, VE), ("S", LAST, 0, SC),
-    ("ZS", "q", 1), ("ZS", "q", 2),
-    ("S", LAST - 1, 2, SC), ("S", LAST - 1, 3, VE),
-    ("ZS", "s", 3), ("ZS", "s", 0),
-    ("S", LAST, 1, SC), ("S", LAST, 2, VE),
-    ("O", LAST - 2, 0, SC), ("O", LAST - 2, 1, SC),
-    ("Z", "s", LAST - 1),
-    ("OS", 3, SC), ("OS", 0, SC),
-    ("ZS", "s", 1), ("ZS", "s", 2),
-    ("O", LAST - 1, 0, VE), ("O", LAST - 1, 1, SC),
-    ("OS", 1, VE), ("OS", 2, SC),
-)
 
 
 def tile_bidirectionalattention_pa_t_kernel(tc, Q, K, V, cos_t, sin_t, out):
@@ -60,7 +39,6 @@ def tile_bidirectionalattention_pa_t_kernel(tc, Q, K, V, cos_t, sin_t, out):
     tab_dram = {"c": cos_t.rearrange("(p r) n -> p (r n)", r=R), "s": sin_t.rearrange("(p r) n -> p (r n)", r=R)}
     v_dram = V.rearrange("b o (p j) d -> p (b o) (j d)", j=R)
     o_dram = out.rearrange("b h (p r) d -> (b h) p (r d)", r=R)
-    HALF = R * N // 2
 
     with ExitStack() as ctx:
         ctx.enter_context(tc.manual_schedule())
@@ -74,17 +52,20 @@ def tile_bidirectionalattention_pa_t_kernel(tc, Q, K, V, cos_t, sin_t, out):
         ps_tab = ctx.enter_context(tc.psum_pool(name="ps_tab", bufs=1))
         ps = ctx.enter_context(tc.psum_pool(name="ps", bufs=5))
 
-        ident = const.tile([P, P], F32, name="ident")
-        make_identity(nc, ident[:])
         ident_bf = const.tile([P, P], BF16, name="ident_bf")
         make_identity(nc, ident_bf[:])
+        minus_bf = const.tile([P, P], BF16, name="minus_bf")
+        nc.vector.tensor_scalar_mul(out=minus_bf[:], in0=ident_bf[:], scalar1=-1.0)
+        ident = const.tile([P, P], F32, name="ident")
+        nc.vector.tensor_copy(out=ident[:], in_=ident_bf[:])
         v_raw = const.tile([P, B, R * D], BF16, name="v_raw")
         v_grp = const.tile([P, B, D, R], BF16, name="v_grp", align_bytes=64)
         v_codes = const.tile([P, B * D], U32, name="v_codes", align_bytes=64)
         v_scales = const.tile([P, B * D], U8, name="v_scales", align_bytes=64)
         gate = const.tile([P, 1], U32, name="gate")
-        tab_raw = {}
-        tabs = {}
+        tab_raw = {nm: const.tile([P, R * N], BF16, name="tab_raw_" + nm) for nm in ("c", "s")}
+        pool_tab = const.tile([P, 2, 2, I], BF16, name="pool_tab")
+        shared_sin = const.tile([P, 2, I], BF16, name="shared_sin")
         tab_ps = {}
         st = {}
 
@@ -93,50 +74,46 @@ def tile_bidirectionalattention_pa_t_kernel(tc, Q, K, V, cos_t, sin_t, out):
             nc.sync.dma_start(out=t[:], in_=dram[nm][g])
             st[(nm, g)] = t
 
-        def load_tables(h):
+        def load_tables(first, count):
+            cols = slice(first * N, (first + count) * N)
             for nm in ("c", "s"):
-                t = const.tile([P, HALF], BF16, name="raw_%s%d" % (nm, h))
-                nc.sync.dma_start(out=t[:], in_=tab_dram[nm][:, h * HALF:(h + 1) * HALF])
-                tab_raw[(nm, h)] = t[:].rearrange("p (r i e) -> p r e i", r=2, e=2)
+                nc.sync.dma_start(out=tab_raw[nm][:, cols], in_=tab_dram[nm][:, cols])
 
-        def prepare_tables(h, eng_cos):
-            t = const.tile([P, 2, 2, 2, I], BF16, name="tabs%d" % h)
-            eng_cos(out=t[:, :, 0, :, :], in_=tab_raw[("c", h)])
-            nc.scalar.copy(out=t[:, :, 1, 0, :], in_=tab_raw[("s", h)][:, :, 1, :])
-            nc.scalar.mul(out=t[:, :, 1, 1, :], in_=tab_raw[("s", h)][:, :, 0, :], mul=-1.0)
-            tabs[h] = t
-
-        def pool_copy(out, in_):
-            nc.gpsimd.tensor_scalar(out=out, in0=in_, scalar1=1.0, scalar2=0.0, op0=MULT, op1=mybir.AluOpType.add)
-
-        def table_sb(r):
-            return tabs[r // 2][:, r % 2, :, :, :]
+        def raw_table(nm, r):
+            return tab_raw[nm][:].rearrange("p (r i e) -> p r e i", r=R, e=2)[:, r, :, :]
 
         def table_to_psum(r):
             tab_ps[r] = ps_tab.tile([P, 2, 2, I], BF16, name="tab_ps%d" % r)
-            for t in range(2):
-                nc.tensor.matmul(out=tab_ps[r][:, t, :, :].rearrange("p e i -> p (e i)"), lhsT=ident_bf[:],
-                                 rhs=table_sb(r)[:, t, :, :].rearrange("p e i -> p (e i)"), start=True, stop=True)
+            for e in range(2):
+                nc.tensor.matmul(out=tab_ps[r][:, 0, e, :], lhsT=ident_bf[:], rhs=raw_table("c", r)[:, e, :], start=True, stop=True)
+            nc.tensor.matmul(out=tab_ps[r][:, 1, 0, :], lhsT=ident_bf[:], rhs=raw_table("s", r)[:, 1, :], start=True, stop=True)
+            nc.tensor.matmul(out=tab_ps[r][:, 1, 1, :], lhsT=minus_bf[:], rhs=raw_table("s", r)[:, 0, :], start=True, stop=True)
+
+        def prepare_pool_tables():
+            nc.scalar.copy(out=pool_tab[:, 0, :, :], in_=raw_table("c", R_POOL))
+            for r, dst in ((R_POOL, pool_tab[:, 1, :, :]), (R_SHARED, shared_sin[:])):
+                nc.scalar.copy(out=dst[:, 0, :], in_=raw_table("s", r)[:, 1, :])
+                nc.scalar.mul(out=dst[:, 1, :], in_=raw_table("s", r)[:, 0, :], mul=-1.0)
 
         def planes(nm, g, r):
             return st[(nm, g)][:].rearrange("p (r i e) -> p r e i", r=R, e=2)[:, r, :, :]
 
+        def pool_sines(nm, g):
+            r = R_SHARED
+            st[(nm, g, r)] = prod_v.tile([P, 2, 2, I], F32, name="ab_s", bufs=3)
+            nc.gpsimd.tensor_tensor(out=st[(nm, g, r)][:, 1, :, :], in0=planes(nm, g, r), in1=shared_sin[:], op=MULT)
+
         def pool_products(nm, g):
             ab = prod_g.tile([P, 2, 2, I], F32, name="ab_g")
-            nc.gpsimd.tensor_tensor(out=ab[:], in0=planes(nm, g, R_POOL).unsqueeze(1).to_broadcast([P, 2, 2, I]), in1=table_sb(R_POOL), op=MULT)
+            nc.gpsimd.tensor_tensor(out=ab[:], in0=planes(nm, g, R_POOL).unsqueeze(1).to_broadcast([P, 2, 2, I]), in1=pool_tab[:], op=MULT)
             st[(nm, g, R_POOL)] = ab
-            if nm == SHARED[0] and g >= SHARE_FROM:
-                r = SHARED[1]
-                st[(nm, g, r)] = prod_v.tile([P, 2, 2, I], F32, name="ab_s", bufs=3)
-                nc.gpsimd.tensor_tensor(out=st[(nm, g, r)][:, 1, :, :], in0=planes(nm, g, r), in1=table_sb(r)[:, 1, :, :], op=MULT)
 
-        def products(nm, g, r, from_sbuf=False):
-            if (nm, r) == SHARED and g >= SHARE_FROM:
+        def products(nm, g, r):
+            if (nm, g, r) in st:
                 nc.vector.tensor_tensor(out=st[(nm, g, r)][:, 0, :, :], in0=planes(nm, g, r), in1=tab_ps[r][:, 0, :, :], op=MULT)
                 return
             ab = prod_v.tile([P, 2, 2, I], F32, name="ab_v")
-            nc.vector.tensor_tensor(out=ab[:], in0=planes(nm, g, r).unsqueeze(1).to_broadcast([P, 2, 2, I]),
-                                    in1=table_sb(r) if from_sbuf else tab_ps[r][:], op=MULT)
+            nc.vector.tensor_tensor(out=ab[:], in0=planes(nm, g, r).unsqueeze(1).to_broadcast([P, 2, 2, I]), in1=tab_ps[r][:], op=MULT)
             st[(nm, g, r)] = ab
 
         def group_tile(nm, g):
@@ -155,9 +132,11 @@ def tile_bidirectionalattention_pa_t_kernel(tc, Q, K, V, cos_t, sin_t, out):
             else:
                 nc.scalar.activation(out=dst, in_=src, func=COPY, scale=scale)
 
-        def transposes(nm, g, r, eng=SC):
+        def transposes(nm, g, r, eng=SC, hold=0):
             ab = st[(nm, g, r)]
             bank = ps.tile([P, 4, P], F32, name="bank")
+            if hold:
+                nc.tensor.matmul(out=bank[:].rearrange("p j c -> p (j c)")[:, 0:hold], lhsT=ident_bf[:], rhs=tab_raw["c"][:, 0:hold], start=True, stop=True)
             for j in range(4):
                 u, e = j // 2, j % 2
                 cols = slice(u * P, (u + 1) * P)
@@ -171,14 +150,11 @@ def tile_bidirectionalattention_pa_t_kernel(tc, Q, K, V, cos_t, sin_t, out):
                                      mxp.tile([P, T], U8, name=nm + "_scales", align_bytes=64))
             return st[(nm + "x", g)]
 
-        def quantise(nm, g, r=None):
+        def quantise(nm, g, first=0, count=R):
             codes, scales = code_tiles(nm, g)
-            gt = group_tile(nm, g)
-            if r is None:
-                nc.vector.quantize_mx(out=codes[:].bitcast(FP8X4), scales=scales[:], in_=gt[:].rearrange("p a c j -> p (a c j)"))
-            else:
-                cols = slice(r * P, (r + 1) * P)
-                nc.vector.quantize_mx(out=codes[:, cols].bitcast(FP8X4), scales=scales[:, cols], in_=gt[:, r, :, :].rearrange("p c j -> p (c j)"))
+            cols = slice(first * P, (first + count) * P)
+            nc.vector.quantize_mx(out=codes[:, cols].bitcast(FP8X4), scales=scales[:, cols],
+                                  in_=group_tile(nm, g)[:, first:first + count, :, :].rearrange("p a c j -> p (a c j)"))
 
         def values(b):
             nc.scalar.copy(out=v_grp[:, b, :, :], in_=v_raw[:, b, :].rearrange("p (j d) -> p d j", j=R))
@@ -214,85 +190,91 @@ def tile_bidirectionalattention_pa_t_kernel(tc, Q, K, V, cos_t, sin_t, out):
         def store(g, first, count):
             nc.sync.dma_start(out=o_dram[g][:, first * D:(first + count) * D], in_=st[("o", g)][:, first:first + count, :].rearrange("p r d -> p (r d)"))
 
-        def warm():
-            wb = ps.tile([P, 512], F32, name="bank")
-            nc.tensor.matmul(out=wb[:], lhsT=ident_bf[:], rhs=table_sb(0)[:, 0, :, :].rearrange("p e i -> p (e i)"), start=True, stop=True)
-
-        load_tables(0)
-        t0 = raw.tile([P, R * N], BF16, name="raw_qk")
-        st[("q", 0)] = t0
-        nc.sync.dma_start(out=t0[:, 0:HALF], in_=dram["q"][0][:, 0:HALF])
-        load_tables(1)
-        nc.sync.dma_start(out=t0[:, HALF:2 * HALF], in_=dram["q"][0][:, HALF:2 * HALF])
+        q0 = raw.tile([P, R * N], BF16, name="raw_qk")
+        st[("q", 0)] = q0
+        for first, count in ((0, 1), (1, 1), (2, 2)):
+            load_tables(first, count)
+            cols = slice(first * N, (first + count) * N)
+            nc.sync.dma_start(out=q0[:, cols], in_=dram["q"][0][:, cols])
+            if first < 2:
+                table_to_psum(first)
         load("k", 0)
+        nc.sync.dma_start(out=v_raw[:], in_=v_dram)
         for g in range(1, AHEAD):
             load("q", g)
             load("k", g)
-        nc.sync.dma_start(out=v_raw[:], in_=v_dram)
-        prepare_tables(0, nc.vector.tensor_copy)
-        table_to_psum(0)
-        table_to_psum(1)
-        prepare_tables(1, pool_copy if POOL_PREP else nc.scalar.copy)
         table_to_psum(2)
+        prepare_pool_tables()
+
+        def step(g):
+            return ("k", "q") if g == LAST else ("q", "k")
 
         for j in range(HEADS):
             last = j == LAST
             if j + AHEAD < HEADS:
                 load("q", j + AHEAD)
                 load("k", j + AHEAD)
-            first_nm, second_nm = ("k", "q") if last else ("q", "k")
-            if j >= 2:
-                nc.gpsimd.tensor_copy(out=gate[:], in_=code_tiles("k", j - 2)[0][:, 0:1])
-            pool_products(first_nm, j)
-            pool_products(second_nm, j)
-            early = EARLY_ORDER and j == 0
-            for r in range(2 if early else 3):
-                products(first_nm, j, r, from_sbuf=(j == 0 and r < 2))
-            if early:
-                products(second_nm, j, 0)
-                products(second_nm, j, 1)
-                products(first_nm, j, 2)
-            for kind, idx, lag in (PE_LAST if last else PE_ORDER):
-                g = j - lag
-                if g < 0:
-                    if WARM and kind in ("s", "o"):
-                        warm()
-                elif kind == "s":
-                    scores(g, idx)
-                    if BURST_DUMMY and idx == 0:
-                        warm()
-                elif kind == "o":
-                    output(g, 2 * idx, 2)
-                    if idx == 1:
-                        store(g, 0, R)
-                else:
-                    transposes(kind, g, idx)
-            if j < B:
-                values(j)
-            for r in range(2 if early else 0, 3):
-                products(second_nm, j, r)
-            if not last:
-                if j >= 2:
-                    quantise("s", j - 2)
-                if j >= 1:
+            nm1, nm2 = step(j)
+            pool_products(nm1, j)
+            for r in range(3):
+                products(nm1, j, r)
+            for what in ORDER:
+                if what == "2" and j >= 1:
+                    for r, h in zip(SEC_TILES, HOLD2):
+                        transposes(step(j - 1)[1], j - 1, r, hold=h)
+                    if j >= 2:
+                        quantise("s", j - 2)
+                    if j == 1:
+                        for b in range(2):
+                            quantise_values(b)
+                    if j == 2:
+                        for b in range(2, B):
+                            quantise_values(b)
                     quantise("q", j - 1)
                     quantise("k", j - 1)
-                if 1 <= j <= B:
-                    quantise_values(j - 1)
+                elif what == "1":
+                    for r, h in zip(TILES, HOLD1):
+                        transposes(nm1, j, r, hold=h)
+                elif what == "s" and j >= 1:
+                    for r in range(R):
+                        scores(j - 1, r)
+                elif what == "o" and j >= 2:
+                    output(j - 2, 0, 2)
+                    output(j - 2, 2, 2)
+                    store(j - 2, 0, R)
+            if j == 0:
+                values(0)
+                values(1)
+            if j == 1:
+                values(2)
+                values(3)
+            if GATE and j >= 1:
+                nc.gpsimd.tensor_copy(out=gate[:], in_=code_tiles("k", j - 1)[0][:, 0:1])
+            pool_products(nm2, j)
+            if not last:
+                pool_sines(nm2, j)
+            for r in range(3):
+                products(nm2, j, r)
 
-        for step in EPILOGUE:
-            if step[0] == "Z":
-                quantise(step[1], step[2])
-            elif step[0] == "ZS":
-                quantise(step[1], LAST, step[2])
-            elif step[0] == "T":
-                transposes(step[1], LAST, step[2], step[3])
-            elif step[0] == "S":
-                scores(step[1], step[2], step[3])
-            elif step[0] == "O":
-                output(step[1], 2 * step[2], 2, step[3])
-                if step[2] == 1:
-                    store(step[1], 0, R)
-            elif step[0] == "OS":
-                output(LAST, step[1], 1, step[2])
-        store(LAST, 0, R)
+        quantise("k", LAST)
+        transposes("q", LAST, 0, VE)
+        transposes("q", LAST, 1, SC)
+        quantise("s", LAST - 1)
+        transposes("q", LAST, 3, VE)
+        transposes("q", LAST, 2, SC)
+        quantise("q", LAST, 0, 2)
+        output(LAST - 1, 0, 2, SC)
+        output(LAST - 1, 2, 2, VE)
+        store(LAST - 1, 0, R)
+        scores(LAST, 0, SC)
+        scores(LAST, 1, VE)
+        quantise("q", LAST, 2, 2)
+        scores(LAST, 2, SC)
+        quantise("s", LAST, 0, 2)
+        scores(LAST, 3, VE)
+        output(LAST, 0, 2, SC)
+        store(LAST, 0, 2)
+        quantise("s", LAST, 2, 2)
+        output(LAST, 2, 1, SC)
+        output(LAST, 3, 1, VE)
+        store(LAST, 2, 2)

@@ -26,8 +26,8 @@ SHARE_FROM = 0
 GATE = True
 TILES = (0, 1, 2, 3)
 SEC_TILES = (3, 0, 1, 2)
-HOLD1 = (256, 0, 256, 0)
-HOLD2 = (0, 0, 256, 0)
+HOLD1 = (0, 0, 0, 0)
+HOLD2 = (0, 0, 0, 0)
 ORDER = ("2", "1", "s", "o")
 SC, VE = "scalar", "vector"
 

@@ -20,14 +20,10 @@ HEADS = B * H
 LAST = HEADS - 1
 FLOPS = HEADS * (2 * T * T * N + 2 * T * T * D)
 AHEAD = 3
-R_POOL = 3
-R_SHARED = 2
-SHARE_FROM = 0
-GATE = True
+G_FIRST = 1
+G_SECOND = 2
 TILES = (0, 1, 2, 3)
-SEC_TILES = (3, 0, 1, 2)
-HOLD1 = (0, 0, 0, 0)
-HOLD2 = (0, 0, 0, 0)
+SEC_TILES = (0, 1, 2, 3)
 ORDER = ("2", "1", "s", "o")
 SC, VE = "scalar", "vector"
 
@@ -47,6 +43,7 @@ def tile_bidirectionalattention_pa_t_kernel(tc, Q, K, V, cos_t, sin_t, out):
         prod_v = ctx.enter_context(tc.tile_pool(name="prod_v", bufs=10))
         prod_g = ctx.enter_context(tc.tile_pool(name="prod_g", bufs=4))
         grp = ctx.enter_context(tc.tile_pool(name="grp", bufs=3))
+        ring = ctx.enter_context(tc.tile_pool(name="ring", bufs=1))
         mxp = ctx.enter_context(tc.tile_pool(name="mxp", bufs=2))
         opool = ctx.enter_context(tc.tile_pool(name="opool", bufs=3))
         ps_tab = ctx.enter_context(tc.psum_pool(name="ps_tab", bufs=1))
@@ -62,12 +59,16 @@ def tile_bidirectionalattention_pa_t_kernel(tc, Q, K, V, cos_t, sin_t, out):
         v_grp = const.tile([P, B, D, R], BF16, name="v_grp", align_bytes=64)
         v_codes = const.tile([P, B * D], U32, name="v_codes", align_bytes=64)
         v_scales = const.tile([P, B * D], U8, name="v_scales", align_bytes=64)
-        gate = const.tile([P, 1], U32, name="gate")
         tab_raw = {nm: const.tile([P, R * N], BF16, name="tab_raw_" + nm) for nm in ("c", "s")}
-        pool_tab = const.tile([P, 2, 2, I], BF16, name="pool_tab")
-        shared_sin = const.tile([P, 2, I], BF16, name="shared_sin")
+        sin_sb = const.tile([P, R - G_FIRST, 2, I], BF16, name="sin_sb")
         tab_ps = {}
         st = {}
+
+        def second_of(g):
+            return "q" if g == LAST else "k"
+
+        def first_of(g):
+            return "k" if g == LAST else "q"
 
         def load(nm, g):
             t = raw.tile([P, R * N], BF16, name="raw_qk")
@@ -82,43 +83,62 @@ def tile_bidirectionalattention_pa_t_kernel(tc, Q, K, V, cos_t, sin_t, out):
         def raw_table(nm, r):
             return tab_raw[nm][:].rearrange("p (r i e) -> p r e i", r=R, e=2)[:, r, :, :]
 
+        def cos_to_psum(dst, r):
+            for e in range(2):
+                nc.tensor.matmul(out=dst[:, e, :], lhsT=ident_bf[:], rhs=raw_table("c", r)[:, e, :], start=True, stop=True)
+
+        def sin_to_psum(dst, r):
+            nc.tensor.matmul(out=dst[:, 0, :], lhsT=ident_bf[:], rhs=raw_table("s", r)[:, 1, :], start=True, stop=True)
+            nc.tensor.matmul(out=dst[:, 1, :], lhsT=minus_bf[:], rhs=raw_table("s", r)[:, 0, :], start=True, stop=True)
+
         def table_to_psum(r):
             tab_ps[r] = ps_tab.tile([P, 2, 2, I], BF16, name="tab_ps%d" % r)
-            for e in range(2):
-                nc.tensor.matmul(out=tab_ps[r][:, 0, e, :], lhsT=ident_bf[:], rhs=raw_table("c", r)[:, e, :], start=True, stop=True)
-            nc.tensor.matmul(out=tab_ps[r][:, 1, 0, :], lhsT=ident_bf[:], rhs=raw_table("s", r)[:, 1, :], start=True, stop=True)
-            nc.tensor.matmul(out=tab_ps[r][:, 1, 1, :], lhsT=minus_bf[:], rhs=raw_table("s", r)[:, 0, :], start=True, stop=True)
+            if r < 2:
+                cos_to_psum(tab_ps[r][:, 0, :, :], r)
+                sin_to_psum(tab_ps[r][:, 1, :, :], r)
+            else:
+                for t in range(2):
+                    cos_to_psum(tab_ps[r][:, t, :, :], r + t)
 
-        def prepare_pool_tables():
-            nc.scalar.copy(out=pool_tab[:, 0, :, :], in_=raw_table("c", R_POOL))
-            for r, dst in ((R_POOL, pool_tab[:, 1, :, :]), (R_SHARED, shared_sin[:])):
-                nc.scalar.copy(out=dst[:, 0, :], in_=raw_table("s", r)[:, 1, :])
-                nc.scalar.mul(out=dst[:, 1, :], in_=raw_table("s", r)[:, 0, :], mul=-1.0)
+        def prepare_sines(first, count):
+            raw_s = tab_raw["s"][:].rearrange("p (r i e) -> p r e i", r=R, e=2)[:, first:first + count, :, :]
+            dst = sin_sb[:, first - G_FIRST:first - G_FIRST + count, :, :]
+            nc.scalar.copy(out=dst[:, :, 0, :], in_=raw_s[:, :, 1, :])
+            nc.scalar.mul(out=dst[:, :, 1, :], in_=raw_s[:, :, 0, :], mul=-1.0)
 
-        def planes(nm, g, r):
-            return st[(nm, g)][:].rearrange("p (r i e) -> p r e i", r=R, e=2)[:, r, :, :]
+        def planes(nm, g, first, count):
+            return st[(nm, g)][:].rearrange("p (r i e) -> p r e i", r=R, e=2)[:, first:first + count, :, :]
 
-        def pool_sines(nm, g):
-            r = R_SHARED
-            st[(nm, g, r)] = prod_v.tile([P, 2, 2, I], F32, name="ab_s", bufs=3)
-            nc.gpsimd.tensor_tensor(out=st[(nm, g, r)][:, 1, :, :], in0=planes(nm, g, r), in1=shared_sin[:], op=MULT)
+        def pool_products(nm, g, first):
+            count = R - first
+            if second_of(g) == nm:
+                ab = ring.tile([P, count, 2, I], F32, name="ring%d" % ((g + 1) % 2), align_bytes=64)
+            else:
+                ab = prod_g.tile([P, count, 2, I], F32, name="ab_g")
+            nc.gpsimd.tensor_tensor(out=ab[:], in0=planes(nm, g, first, count), in1=sin_sb[:, first - G_FIRST:, :, :], op=MULT)
+            for r in range(first, R):
+                st[(nm, g, "s", r)] = ab[:, r - first, :, :]
 
-        def pool_products(nm, g):
-            ab = prod_g.tile([P, 2, 2, I], F32, name="ab_g")
-            nc.gpsimd.tensor_tensor(out=ab[:], in0=planes(nm, g, R_POOL).unsqueeze(1).to_broadcast([P, 2, 2, I]), in1=pool_tab[:], op=MULT)
-            st[(nm, g, R_POOL)] = ab
-
-        def products(nm, g, r):
-            if (nm, g, r) in st:
-                nc.vector.tensor_tensor(out=st[(nm, g, r)][:, 0, :, :], in0=planes(nm, g, r), in1=tab_ps[r][:, 0, :, :], op=MULT)
-                return
+        def products(nm, g, unit, pool_first):
             ab = prod_v.tile([P, 2, 2, I], F32, name="ab_v")
-            nc.vector.tensor_tensor(out=ab[:], in0=planes(nm, g, r).unsqueeze(1).to_broadcast([P, 2, 2, I]), in1=tab_ps[r][:], op=MULT)
-            st[(nm, g, r)] = ab
+            if unit == 2:
+                nc.vector.tensor_tensor(out=ab[:], in0=planes(nm, g, 2, 2), in1=tab_ps[2][:], op=MULT)
+                for t in range(2):
+                    st[(nm, g, "c", 2 + t)] = ab[:, t, :, :]
+            elif unit >= pool_first:
+                nc.vector.tensor_tensor(out=ab[:, 0, :, :], in0=planes(nm, g, unit, 1)[:, 0, :, :], in1=tab_ps[unit][:, 0, :, :], op=MULT)
+                st[(nm, g, "c", unit)] = ab[:, 0, :, :]
+            else:
+                nc.vector.tensor_tensor(out=ab[:], in0=planes(nm, g, unit, 1).to_broadcast([P, 2, 2, I]), in1=tab_ps[unit][:], op=MULT)
+                st[(nm, g, "c", unit)] = ab[:, 0, :, :]
+                st[(nm, g, "s", unit)] = ab[:, 1, :, :]
 
         def group_tile(nm, g):
             if (nm + "g", g) not in st:
-                st[(nm + "g", g)] = grp.tile([P, R, P, 4], BF16, name="grp_" + nm, align_bytes=64)
+                if nm == second_of(g):
+                    st[(nm + "g", g)] = ring.tile([P, R, P, 4], BF16, name="ring%d" % (g % 2), align_bytes=64)
+                else:
+                    st[(nm + "g", g)] = grp.tile([P, R, P, 4], BF16, name="grp_" + nm, align_bytes=64)
             return st[(nm + "g", g)]
 
         def leave_psum(dst, src, scale, eng):
@@ -132,16 +152,13 @@ def tile_bidirectionalattention_pa_t_kernel(tc, Q, K, V, cos_t, sin_t, out):
             else:
                 nc.scalar.activation(out=dst, in_=src, func=COPY, scale=scale)
 
-        def transposes(nm, g, r, eng=SC, hold=0):
-            ab = st[(nm, g, r)]
+        def transposes(nm, g, r, eng=SC):
             bank = ps.tile([P, 4, P], F32, name="bank")
-            if hold:
-                nc.tensor.matmul(out=bank[:].rearrange("p j c -> p (j c)")[:, 0:hold], lhsT=ident_bf[:], rhs=tab_raw["c"][:, 0:hold], start=True, stop=True)
             for j in range(4):
                 u, e = j // 2, j % 2
                 cols = slice(u * P, (u + 1) * P)
-                nc.tensor.matmul(out=bank[:, j, :], lhsT=ab[:, 0, e, cols], rhs=ident[:], is_transpose=True, start=True, stop=False)
-                nc.tensor.matmul(out=bank[:, j, :], lhsT=ab[:, 1, 1 - e, cols], rhs=ident[:], is_transpose=True, start=False, stop=True)
+                nc.tensor.matmul(out=bank[:, j, :], lhsT=st[(nm, g, "c", r)][:, e, cols], rhs=ident[:], is_transpose=True, start=True, stop=False)
+                nc.tensor.matmul(out=bank[:, j, :], lhsT=st[(nm, g, "s", r)][:, 1 - e, cols], rhs=ident[:], is_transpose=True, start=False, stop=True)
             leave_psum(group_tile(nm, g)[:, r, :, :], bank[:].rearrange("p j c -> p c j"), None, eng)
 
         def code_tiles(nm, g):
@@ -204,24 +221,23 @@ def tile_bidirectionalattention_pa_t_kernel(tc, Q, K, V, cos_t, sin_t, out):
             load("q", g)
             load("k", g)
         table_to_psum(2)
-        prepare_pool_tables()
-
-        def step(g):
-            return ("k", "q") if g == LAST else ("q", "k")
+        prepare_sines(2, 2)
+        prepare_sines(1, 1)
 
         for j in range(HEADS):
             last = j == LAST
             if j + AHEAD < HEADS:
                 load("q", j + AHEAD)
                 load("k", j + AHEAD)
-            nm1, nm2 = step(j)
-            pool_products(nm1, j)
-            for r in range(3):
-                products(nm1, j, r)
+            nm1, nm2 = first_of(j), second_of(j)
+            pool_first = G_FIRST if j > 0 else G_SECOND
+            pool_products(nm1, j, pool_first)
+            for unit in range(3):
+                products(nm1, j, unit, pool_first)
             for what in ORDER:
                 if what == "2" and j >= 1:
-                    for r, h in zip(SEC_TILES, HOLD2):
-                        transposes(step(j - 1)[1], j - 1, r, hold=h)
+                    for r in SEC_TILES:
+                        transposes(second_of(j - 1), j - 1, r)
                     if j >= 2:
                         quantise("s", j - 2)
                     if j == 1:
@@ -233,12 +249,12 @@ def tile_bidirectionalattention_pa_t_kernel(tc, Q, K, V, cos_t, sin_t, out):
                     quantise("q", j - 1)
                     quantise("k", j - 1)
                 elif what == "1":
-                    for r, h in zip(TILES, HOLD1):
-                        transposes(nm1, j, r, hold=h)
+                    for r in TILES:
+                        transposes(nm1, j, r)
                 elif what == "s" and j >= 1:
                     for r in range(R):
                         scores(j - 1, r)
-                elif what == "o" and j >= 2:
+                elif what == "o" and 2 <= j < LAST:
                     output(j - 2, 0, 2)
                     output(j - 2, 2, 2)
                     store(j - 2, 0, R)
@@ -248,27 +264,26 @@ def tile_bidirectionalattention_pa_t_kernel(tc, Q, K, V, cos_t, sin_t, out):
             if j == 1:
                 values(2)
                 values(3)
-            if GATE and j >= 1:
-                nc.gpsimd.tensor_copy(out=gate[:], in_=code_tiles("k", j - 1)[0][:, 0:1])
-            pool_products(nm2, j)
-            if not last:
-                pool_sines(nm2, j)
-            for r in range(3):
-                products(nm2, j, r)
+            pool_products(nm2, j, G_SECOND)
+            for unit in range(3):
+                products(nm2, j, unit, G_SECOND)
 
         quantise("k", LAST)
-        transposes("q", LAST, 0, VE)
+        transposes("q", LAST, 0, SC)
         transposes("q", LAST, 1, SC)
-        quantise("s", LAST - 1)
         transposes("q", LAST, 3, VE)
-        transposes("q", LAST, 2, SC)
+        quantise("s", LAST - 1)
         quantise("q", LAST, 0, 2)
-        output(LAST - 1, 0, 2, SC)
-        output(LAST - 1, 2, 2, VE)
-        store(LAST - 1, 0, R)
+        transposes("q", LAST, 2, SC)
+        output(LAST - 2, 0, 2, SC)
+        output(LAST - 2, 2, 2, VE)
+        store(LAST - 2, 0, R)
         scores(LAST, 0, SC)
         scores(LAST, 1, VE)
         quantise("q", LAST, 2, 2)
+        output(LAST - 1, 0, 2, SC)
+        output(LAST - 1, 2, 2, VE)
+        store(LAST - 1, 0, R)
         scores(LAST, 2, SC)
         quantise("s", LAST, 0, 2)
         scores(LAST, 3, VE)
@@ -276,5 +291,6 @@ def tile_bidirectionalattention_pa_t_kernel(tc, Q, K, V, cos_t, sin_t, out):
         store(LAST, 0, 2)
         quantise("s", LAST, 2, 2)
         output(LAST, 2, 1, SC)
+        store(LAST, 2, 1)
         output(LAST, 3, 1, VE)
-        store(LAST, 2, 2)
+        store(LAST, 3, 1)

@@ -17,6 +17,8 @@ P = 128
 R = T // P
 I = N // 2
 HEADS = B * H
+VALUES_AT = {0: (1,), 1: (2, 3)}
+MIDVAL = 1
 LAST = HEADS - 1
 FLOPS = HEADS * (2 * T * T * N + 2 * T * T * D)
 AHEAD = 3
@@ -24,7 +26,7 @@ G_FIRST = 1
 G_SECOND = 2
 TILES = (0, 1, 2, 3)
 SEC_TILES = (0, 1, 2, 3)
-ORDER = ("2", "1", "s", "o")
+ORDER = ("2", "1", "o", "s")
 SC, VE = "scalar", "vector"
 
 
@@ -75,11 +77,6 @@ def tile_bidirectionalattention_pa_t_kernel(tc, Q, K, V, cos_t, sin_t, out):
             nc.sync.dma_start(out=t[:], in_=dram[nm][g])
             st[(nm, g)] = t
 
-        def load_tables(first, count):
-            cols = slice(first * N, (first + count) * N)
-            for nm in ("c", "s"):
-                nc.sync.dma_start(out=tab_raw[nm][:, cols], in_=tab_dram[nm][:, cols])
-
         def raw_table(nm, r):
             return tab_raw[nm][:].rearrange("p (r i e) -> p r e i", r=R, e=2)[:, r, :, :]
 
@@ -104,7 +101,7 @@ def tile_bidirectionalattention_pa_t_kernel(tc, Q, K, V, cos_t, sin_t, out):
             raw_s = tab_raw["s"][:].rearrange("p (r i e) -> p r e i", r=R, e=2)[:, first:first + count, :, :]
             dst = sin_sb[:, first - G_FIRST:first - G_FIRST + count, :, :]
             nc.scalar.copy(out=dst[:, :, 0, :], in_=raw_s[:, :, 1, :])
-            nc.scalar.mul(out=dst[:, :, 1, :], in_=raw_s[:, :, 0, :], mul=-1.0)
+            nc.gpsimd.tensor_scalar(out=dst[:, :, 1, :], in0=raw_s[:, :, 0, :], scalar1=-1.0, scalar2=0.0, op0=MULT, op1=mybir.AluOpType.add)
 
         def planes(nm, g, first, count):
             return st[(nm, g)][:].rearrange("p (r i e) -> p r e i", r=R, e=2)[:, first:first + count, :, :]
@@ -129,7 +126,11 @@ def tile_bidirectionalattention_pa_t_kernel(tc, Q, K, V, cos_t, sin_t, out):
                 nc.vector.tensor_tensor(out=ab[:, 0, :, :], in0=planes(nm, g, unit, 1)[:, 0, :, :], in1=tab_ps[unit][:, 0, :, :], op=MULT)
                 st[(nm, g, "c", unit)] = ab[:, 0, :, :]
             else:
-                nc.vector.tensor_tensor(out=ab[:], in0=planes(nm, g, unit, 1).to_broadcast([P, 2, 2, I]), in1=tab_ps[unit][:], op=MULT)
+                if nm == "q" and g == 0 and unit == 0:
+                    for t in range(2):
+                        nc.vector.tensor_tensor(out=ab[:, t, :, :], in0=planes(nm, g, unit, 1)[:, 0, :, :], in1=tab_ps[unit][:, t, :, :], op=MULT)
+                else:
+                    nc.vector.tensor_tensor(out=ab[:], in0=planes(nm, g, unit, 1).to_broadcast([P, 2, 2, I]), in1=tab_ps[unit][:], op=MULT)
                 st[(nm, g, "c", unit)] = ab[:, 0, :, :]
                 st[(nm, g, "s", unit)] = ab[:, 1, :, :]
 
@@ -209,20 +210,24 @@ def tile_bidirectionalattention_pa_t_kernel(tc, Q, K, V, cos_t, sin_t, out):
 
         q0 = raw.tile([P, R * N], BF16, name="raw_qk")
         st[("q", 0)] = q0
-        for first, count in ((0, 1), (1, 1), (2, 2)):
-            load_tables(first, count)
+        for first, count in ((0, 1), (2, 2), (1, 1)):
             cols = slice(first * N, (first + count) * N)
-            nc.sync.dma_start(out=q0[:, cols], in_=dram["q"][0][:, cols])
-            if first < 2:
-                table_to_psum(first)
+            nc.scalar.dma_start(out=q0[:, cols], in_=dram["q"][0][:, cols])
+        for nm, first, count in (("c", 0, 1), ("s", 0, 1), ("s", 2, 2), ("c", 1, 1), ("s", 1, 1), ("c", 2, 2)):
+            cols = slice(first * N, (first + count) * N)
+            nc.sync.dma_start(out=tab_raw[nm][:, cols], in_=tab_dram[nm][:, cols])
+        table_to_psum(0)
+        table_to_psum(1)
+        if MIDVAL >= 0:
+            nc.sync.dma_start(out=v_raw[:, 0, :], in_=v_dram[:, 0, :])
         load("k", 0)
-        nc.sync.dma_start(out=v_raw[:], in_=v_dram)
+        rest = 1 if MIDVAL >= 0 else 0
+        nc.sync.dma_start(out=v_raw[:, rest:, :], in_=v_dram[:, rest:, :])
         for g in range(1, AHEAD):
             load("q", g)
             load("k", g)
         table_to_psum(2)
         prepare_sines(2, 2)
-        prepare_sines(1, 1)
 
         for j in range(HEADS):
             last = j == LAST
@@ -232,6 +237,8 @@ def tile_bidirectionalattention_pa_t_kernel(tc, Q, K, V, cos_t, sin_t, out):
             nm1, nm2 = first_of(j), second_of(j)
             pool_first = G_FIRST if j > 0 else G_SECOND
             pool_products(nm1, j, pool_first)
+            if j == 0:
+                prepare_sines(1, 1)
             for unit in range(3):
                 products(nm1, j, unit, pool_first)
             for what in ORDER:
@@ -240,17 +247,17 @@ def tile_bidirectionalattention_pa_t_kernel(tc, Q, K, V, cos_t, sin_t, out):
                         transposes(second_of(j - 1), j - 1, r)
                     if j >= 2:
                         quantise("s", j - 2)
-                    if j == 1:
-                        for b in range(2):
-                            quantise_values(b)
-                    if j == 2:
-                        for b in range(2, B):
-                            quantise_values(b)
+                    for b in VALUES_AT.get(j - 1, ()):
+                        quantise_values(b)
+                    if j == 1 and MIDVAL >= 0:
+                        quantise_values(0)
                     quantise("q", j - 1)
                     quantise("k", j - 1)
                 elif what == "1":
                     for r in TILES:
                         transposes(nm1, j, r)
+                        if j == 0 and r == MIDVAL:
+                            values(0)
                 elif what == "s" and j >= 1:
                     for r in range(R):
                         scores(j - 1, r)
@@ -258,12 +265,8 @@ def tile_bidirectionalattention_pa_t_kernel(tc, Q, K, V, cos_t, sin_t, out):
                     output(j - 2, 0, 2)
                     output(j - 2, 2, 2)
                     store(j - 2, 0, R)
-            if j == 0:
-                values(0)
-                values(1)
-            if j == 1:
-                values(2)
-                values(3)
+            for b in VALUES_AT.get(j, ()):
+                values(b)
             pool_products(nm2, j, G_SECOND)
             for unit in range(3):
                 products(nm2, j, unit, G_SECOND)
@@ -271,25 +274,26 @@ def tile_bidirectionalattention_pa_t_kernel(tc, Q, K, V, cos_t, sin_t, out):
         quantise("k", LAST)
         transposes("q", LAST, 0, SC)
         transposes("q", LAST, 1, SC)
-        transposes("q", LAST, 3, VE)
         quantise("s", LAST - 1)
         quantise("q", LAST, 0, 2)
+        transposes("q", LAST, 3, VE)
         transposes("q", LAST, 2, SC)
-        output(LAST - 2, 0, 2, SC)
-        output(LAST - 2, 2, 2, VE)
-        store(LAST - 2, 0, R)
         scores(LAST, 0, SC)
         scores(LAST, 1, VE)
+        output(LAST - 2, 0, 2, SC)
         quantise("q", LAST, 2, 2)
+        output(LAST - 2, 2, 2, VE)
+        store(LAST - 2, 0, R)
         output(LAST - 1, 0, 2, SC)
-        output(LAST - 1, 2, 2, VE)
-        store(LAST - 1, 0, R)
+        store(LAST - 1, 0, 2)
         scores(LAST, 2, SC)
         quantise("s", LAST, 0, 2)
         scores(LAST, 3, VE)
         output(LAST, 0, 2, SC)
         store(LAST, 0, 2)
         quantise("s", LAST, 2, 2)
+        output(LAST - 1, 2, 2, VE)
+        store(LAST - 1, 2, 2)
         output(LAST, 2, 1, SC)
         store(LAST, 2, 1)
         output(LAST, 3, 1, VE)

@@ -17,7 +17,7 @@ P = 128
 R = T // P
 I = N // 2
 HEADS = B * H
-VALUES_AT = {0: (1,), 1: (2, 3)}
+VALUES_AT = {0: (1,), 1: (2,), 2: (3,)}
 MIDVAL = 1
 LAST = HEADS - 1
 FLOPS = HEADS * (2 * T * T * N + 2 * T * T * D)
@@ -108,13 +108,19 @@ def tile_bidirectionalattention_pa_t_kernel(tc, Q, K, V, cos_t, sin_t, out):
 
         def pool_products(nm, g, first):
             count = R - first
-            if second_of(g) == nm:
-                ab = ring.tile([P, count, 2, I], F32, name="ring%d" % ((g + 1) % 2), align_bytes=64)
+            if first_of(g) == nm:
+                ab = ring.tile([P, count, 2, I], F32, name="ring%d" % (g % 2), align_bytes=64)
             else:
                 ab = prod_g.tile([P, count, 2, I], F32, name="ab_g")
             nc.gpsimd.tensor_tensor(out=ab[:], in0=planes(nm, g, first, count), in1=sin_sb[:, first - G_FIRST:, :, :], op=MULT)
             for r in range(first, R):
                 st[(nm, g, "s", r)] = ab[:, r - first, :, :]
+
+        def sines(nm, g):
+            ab = prod_v.tile([P, 2, 2, I], F32, name="ab_v")
+            nc.vector.tensor_tensor(out=ab[:], in0=planes(nm, g, G_SECOND, R - G_SECOND), in1=sin_sb[:, G_SECOND - G_FIRST:, :, :], op=MULT)
+            for r in range(G_SECOND, R):
+                st[(nm, g, "s", r)] = ab[:, r - G_SECOND, :, :]
 
         def products(nm, g, unit, pool_first):
             ab = prod_v.tile([P, 2, 2, I], F32, name="ab_v")
@@ -236,11 +242,15 @@ def tile_bidirectionalattention_pa_t_kernel(tc, Q, K, V, cos_t, sin_t, out):
                 load("k", j + AHEAD)
             nm1, nm2 = first_of(j), second_of(j)
             pool_first = G_FIRST if j > 0 else G_SECOND
-            pool_products(nm1, j, pool_first)
             if j == 0:
+                pool_products(nm1, j, pool_first)
                 prepare_sines(1, 1)
+                pool_products(nm2, j, G_SECOND)
+                pool_products(first_of(1), 1, G_FIRST)
             for unit in range(3):
                 products(nm1, j, unit, pool_first)
+            if j == 1:
+                sines(nm2, j)
             for what in ORDER:
                 if what == "2" and j >= 1:
                     for r in SEC_TILES:
@@ -267,7 +277,9 @@ def tile_bidirectionalattention_pa_t_kernel(tc, Q, K, V, cos_t, sin_t, out):
                     store(j - 2, 0, R)
             for b in VALUES_AT.get(j, ()):
                 values(b)
-            pool_products(nm2, j, G_SECOND)
+            if 0 < j < LAST:
+                pool_products(first_of(j + 1), j + 1, G_FIRST)
+                pool_products(second_of(j + 1), j + 1, G_SECOND)
             for unit in range(3):
                 products(nm2, j, unit, G_SECOND)
 

from contextlib import ExitStack
import math

import concourse.mybir as mybir
from concourse.masks import make_identity

F32 = mybir.dt.float32
BF16 = mybir.dt.bfloat16
U32 = mybir.dt.uint32
U8 = mybir.dt.uint8
FP8X4 = mybir.dt.float8_e4m3fn_x4
MULT = mybir.AluOpType.mult
COPY = mybir.ActivationFunctionType.Copy

B, H, T, N, D = 4, 4, 512, 512, 256
P = 128
R = T // P
I = N // 2
HEADS = B * H
VALUES_AT = {0: (1,), 1: (2,), 2: (3,)}
MIDVAL = 1
LAST = HEADS - 1
FLOPS = HEADS * (2 * T * T * N + 2 * T * T * D)
AHEAD = 3
G_FIRST = 1
G_SECOND = 2
TILES = (0, 1, 2, 3)
SEC_TILES = (0, 1, 2, 3)
ORDER = ("2", "1", "o", "s")
SC, VE = "scalar", "vector"


def tile_bidirectionalattention_pa_t_kernel(tc, Q, K, V, cos_t, sin_t, out):
    nc = tc.nc
    inv_sqrt_n = 1.0 / math.sqrt(N)
    dram = {"q": Q.rearrange("b h (p r) n -> (b h) p (r n)", r=R), "k": K.rearrange("b h (p r) n -> (b h) p (r n)", r=R)}
    tab_dram = {"c": cos_t.rearrange("(p r) n -> p (r n)", r=R), "s": sin_t.rearrange("(p r) n -> p (r n)", r=R)}
    v_dram = V.rearrange("b o (p j) d -> p (b o) (j d)", j=R)
    o_dram = out.rearrange("b h (p r) d -> (b h) p (r d)", r=R)

    with ExitStack() as ctx:
        ctx.enter_context(tc.manual_schedule())
        const = ctx.enter_context(tc.tile_pool(name="const", bufs=1))
        raw = ctx.enter_context(tc.tile_pool(name="raw", bufs=2 * (AHEAD + 1)))
        prod_v = ctx.enter_context(tc.tile_pool(name="prod_v", bufs=10))
        prod_g = ctx.enter_context(tc.tile_pool(name="prod_g", bufs=4))
        grp = ctx.enter_context(tc.tile_pool(name="grp", bufs=3))
        ring = ctx.enter_context(tc.tile_pool(name="ring", bufs=1))
        mxp = ctx.enter_context(tc.tile_pool(name="mxp", bufs=2))
        opool = ctx.enter_context(tc.tile_pool(name="opool", bufs=3))
        ps_tab = ctx.enter_context(tc.psum_pool(name="ps_tab", bufs=1))
        ps = ctx.enter_context(tc.psum_pool(name="ps", bufs=5))

        ident_bf = const.tile([P, P], BF16, name="ident_bf")
        make_identity(nc, ident_bf[:])
        minus_bf = const.tile([P, P], BF16, name="minus_bf")
        nc.vector.tensor_scalar_mul(out=minus_bf[:], in0=ident_bf[:], scalar1=-1.0)
        ident = const.tile([P, P], F32, name="ident")
        nc.vector.tensor_copy(out=ident[:], in_=ident_bf[:])
        v_raw = const.tile([P, B, R * D], BF16, name="v_raw")
        v_grp = const.tile([P, B, D, R], BF16, name="v_grp", align_bytes=64)
        v_codes = const.tile([P, B * D], U32, name="v_codes", align_bytes=64)
        v_scales = const.tile([P, B * D], U8, name="v_scales", align_bytes=64)
        tab_raw = {nm: const.tile([P, R * N], BF16, name="tab_raw_" + nm) for nm in ("c", "s")}
        sin_sb = const.tile([P, R - G_FIRST, 2, I], BF16, name="sin_sb")
        tab_ps = {}
        st = {}

        def second_of(g):
            return "q" if g == LAST else "k"

        def first_of(g):
            return "k" if g == LAST else "q"

        def load(nm, g):
            t = raw.tile([P, R * N], BF16, name="raw_qk")
            nc.sync.dma_start(out=t[:], in_=dram[nm][g])
            st[(nm, g)] = t

        def raw_table(nm, r):
            return tab_raw[nm][:].rearrange("p (r i e) -> p r e i", r=R, e=2)[:, r, :, :]

        def cos_to_psum(dst, r):
            for e in range(2):
                nc.tensor.matmul(out=dst[:, e, :], lhsT=ident_bf[:], rhs=raw_table("c", r)[:, e, :], start=True, stop=True)

        def sin_to_psum(dst, r):
            nc.tensor.matmul(out=dst[:, 0, :], lhsT=ident_bf[:], rhs=raw_table("s", r)[:, 1, :], start=True, stop=True)
            nc.tensor.matmul(out=dst[:, 1, :], lhsT=minus_bf[:], rhs=raw_table("s", r)[:, 0, :], start=True, stop=True)

        def table_to_psum(r):
            tab_ps[r] = ps_tab.tile([P, 2, 2, I], BF16, name="tab_ps%d" % r)
            if r < 2:
                cos_to_psum(tab_ps[r][:, 0, :, :], r)
                sin_to_psum(tab_ps[r][:, 1, :, :], r)
            else:
                for t in range(2):
                    cos_to_psum(tab_ps[r][:, t, :, :], r + t)

        def prepare_sines(first, count):
            raw_s = tab_raw["s"][:].rearrange("p (r i e) -> p r e i", r=R, e=2)[:, first:first + count, :, :]
            dst = sin_sb[:, first - G_FIRST:first - G_FIRST + count, :, :]
            nc.scalar.copy(out=dst[:, :, 0, :], in_=raw_s[:, :, 1, :])
            nc.gpsimd.tensor_scalar(out=dst[:, :, 1, :], in0=raw_s[:, :, 0, :], scalar1=-1.0, scalar2=0.0, op0=MULT, op1=mybir.AluOpType.add)

        def planes(nm, g, first, count):
            return st[(nm, g)][:].rearrange("p (r i e) -> p r e i", r=R, e=2)[:, first:first + count, :, :]

        def pool_products(nm, g, first):
            count = R - first
            if first_of(g) == nm:
                ab = ring.tile([P, count, 2, I], F32, name="ring%d" % (g % 2), align_bytes=64)
            else:
                ab = prod_g.tile([P, count, 2, I], F32, name="ab_g")
            nc.gpsimd.tensor_tensor(out=ab[:], in0=planes(nm, g, first, count), in1=sin_sb[:, first - G_FIRST:, :, :], op=MULT)
            for r in range(first, R):
                st[(nm, g, "s", r)] = ab[:, r - first, :, :]

        def sines(nm, g):
            ab = prod_v.tile([P, 2, 2, I], F32, name="ab_v")
            nc.vector.tensor_tensor(out=ab[:], in0=planes(nm, g, G_SECOND, R - G_SECOND), in1=sin_sb[:, G_SECOND - G_FIRST:, :, :], op=MULT)
            for r in range(G_SECOND, R):
                st[(nm, g, "s", r)] = ab[:, r - G_SECOND, :, :]

        def products(nm, g, unit, pool_first):
            ab = prod_v.tile([P, 2, 2, I], F32, name="ab_v")
            if unit == 2:
                nc.vector.tensor_tensor(out=ab[:], in0=planes(nm, g, 2, 2), in1=tab_ps[2][:], op=MULT)
                for t in range(2):
                    st[(nm, g, "c", 2 + t)] = ab[:, t, :, :]
            elif unit >= pool_first:
                nc.vector.tensor_tensor(out=ab[:, 0, :, :], in0=planes(nm, g, unit, 1)[:, 0, :, :], in1=tab_ps[unit][:, 0, :, :], op=MULT)
                st[(nm, g, "c", unit)] = ab[:, 0, :, :]
            else:
                if nm == "q" and g == 0 and unit == 0:
                    for t in range(2):
                        nc.vector.tensor_tensor(out=ab[:, t, :, :], in0=planes(nm, g, unit, 1)[:, 0, :, :], in1=tab_ps[unit][:, t, :, :], op=MULT)
                else:
                    nc.vector.tensor_tensor(out=ab[:], in0=planes(nm, g, unit, 1).to_broadcast([P, 2, 2, I]), in1=tab_ps[unit][:], op=MULT)
                st[(nm, g, "c", unit)] = ab[:, 0, :, :]
                st[(nm, g, "s", unit)] = ab[:, 1, :, :]

        def group_tile(nm, g):
            if (nm + "g", g) not in st:
                if nm == second_of(g):
                    st[(nm + "g", g)] = ring.tile([P, R, P, 4], BF16, name="ring%d" % (g % 2), align_bytes=64)
                else:
                    st[(nm + "g", g)] = grp.tile([P, R, P, 4], BF16, name="grp_" + nm, align_bytes=64)
            return st[(nm + "g", g)]

        def leave_psum(dst, src, scale, eng):
            if eng == VE:
                if scale is None:
                    nc.vector.tensor_copy(out=dst, in_=src)
                else:
                    nc.vector.tensor_scalar_mul(out=dst, in0=src, scalar1=scale)
            elif scale is None:
                nc.scalar.copy(out=dst, in_=src)
            else:
                nc.scalar.activation(out=dst, in_=src, func=COPY, scale=scale)

        def transposes(nm, g, r, eng=SC):
            bank = ps.tile([P, 4, P], F32, name="bank")
            for j in range(4):
                u, e = j // 2, j % 2
                cols = slice(u * P, (u + 1) * P)
                nc.tensor.matmul(out=bank[:, j, :], lhsT=st[(nm, g, "c", r)][:, e, cols], rhs=ident[:], is_transpose=True, start=True, stop=False)
                nc.tensor.matmul(out=bank[:, j, :], lhsT=st[(nm, g, "s", r)][:, 1 - e, cols], rhs=ident[:], is_transpose=True, start=False, stop=True)
            leave_psum(group_tile(nm, g)[:, r, :, :], bank[:].rearrange("p j c -> p c j"), None, eng)

        def code_tiles(nm, g):
            if (nm + "x", g) not in st:
                st[(nm + "x", g)] = (mxp.tile([P, T], U32, name=nm + "_codes", align_bytes=64),
                                     mxp.tile([P, T], U8, name=nm + "_scales", align_bytes=64))
            return st[(nm + "x", g)]

        def quantise(nm, g, first=0, count=R):
            codes, scales = code_tiles(nm, g)
            cols = slice(first * P, (first + count) * P)
            nc.vector.quantize_mx(out=codes[:, cols].bitcast(FP8X4), scales=scales[:, cols],
                                  in_=group_tile(nm, g)[:, first:first + count, :, :].rearrange("p a c j -> p (a c j)"))

        def values(b):
            nc.scalar.copy(out=v_grp[:, b, :, :], in_=v_raw[:, b, :].rearrange("p (j d) -> p d j", j=R))

        def quantise_values(b):
            cols = slice(b * D, (b + 1) * D)
            nc.vector.quantize_mx(out=v_codes[:, cols].bitcast(FP8X4), scales=v_scales[:, cols], in_=v_grp[:, b, :, :].rearrange("p d j -> p (d j)"))

        def scores(g, rq, eng=SC):
            qc, qs = code_tiles("q", g)
            kc, ks = code_tiles("k", g)
            bank = ps.tile([P, R, P], F32, name="bank")
            qcols = slice(rq * P, (rq + 1) * P)
            for rk in range(R):
                kcols = slice(rk * P, (rk + 1) * P)
                nc.tensor.matmul_mx(out=bank[:, rk, :], lhsT=kc[:, kcols].bitcast(FP8X4), lhsT_scale=ks[:, kcols],
                                    rhs=qc[:, qcols].bitcast(FP8X4), rhs_scale=qs[:, qcols], start=True, stop=True)
            leave_psum(group_tile("s", g)[:, rq, :, :], bank[:].rearrange("p k c -> p c k"), inv_sqrt_n, eng)

        def output(g, first, count, eng=SC):
            sc, ss = code_tiles("s", g)
            vcols = slice((g // H) * D, (g // H + 1) * D)
            if ("o", g) not in st:
                st[("o", g)] = opool.tile([P, R, D], F32, name="o_sb")
            ot = st[("o", g)]
            bank = ps.tile([P, 2, D], F32, name="bank")
            for w in range(count):
                cols = slice((first + w) * P, (first + w + 1) * P)
                nc.tensor.matmul_mx(out=bank[:, w, :], lhsT=sc[:, cols].bitcast(FP8X4), lhsT_scale=ss[:, cols],
                                    rhs=v_codes[:, vcols].bitcast(FP8X4), rhs_scale=v_scales[:, vcols], start=True, stop=True)
            leave_psum(ot[:, first:first + count, :], bank[:, 0:count, :], None, eng)

        def store(g, first, count):
            nc.sync.dma_start(out=o_dram[g][:, first * D:(first + count) * D], in_=st[("o", g)][:, first:first + count, :].rearrange("p r d -> p (r d)"))

        q0 = raw.tile([P, R * N], BF16, name="raw_qk")
        st[("q", 0)] = q0
        for first, count in ((0, 1), (2, 2), (1, 1)):
            cols = slice(first * N, (first + count) * N)
            nc.scalar.dma_start(out=q0[:, cols], in_=dram["q"][0][:, cols])
        for nm, first, count in (("c", 0, 1), ("s", 0, 1), ("s", 2, 2), ("c", 1, 1), ("s", 1, 1), ("c", 2, 2)):
            cols = slice(first * N, (first + count) * N)
            nc.sync.dma_start(out=tab_raw[nm][:, cols], in_=tab_dram[nm][:, cols])
        table_to_psum(0)
        table_to_psum(1)
        if MIDVAL >= 0:
            nc.sync.dma_start(out=v_raw[:, 0, :], in_=v_dram[:, 0, :])
        load("k", 0)
        rest = 1 if MIDVAL >= 0 else 0
        nc.sync.dma_start(out=v_raw[:, rest:, :], in_=v_dram[:, rest:, :])
        for g in range(1, AHEAD):
            load("q", g)
            load("k", g)
        table_to_psum(2)
        prepare_sines(2, 2)

        for j in range(HEADS):
            last = j == LAST
            if j + AHEAD < HEADS:
                load("q", j + AHEAD)
                load("k", j + AHEAD)
            nm1, nm2 = first_of(j), second_of(j)
            pool_first = G_FIRST if j > 0 else G_SECOND
            if j == 0:
                pool_products(nm1, j, pool_first)
                prepare_sines(1, 1)
                pool_products(nm2, j, G_SECOND)
                pool_products(first_of(1), 1, G_FIRST)
            for unit in range(3):
                products(nm1, j, unit, pool_first)
            if j == 1:
                sines(nm2, j)
            for what in ORDER:
                if what == "2" and j >= 1:
                    for r in SEC_TILES:
                        transposes(second_of(j - 1), j - 1, r)
                    if j >= 2:
                        quantise("s", j - 2)
                    for b in VALUES_AT.get(j - 1, ()):
                        quantise_values(b)
                    if j == 1 and MIDVAL >= 0:
                        quantise_values(0)
                    quantise("q", j - 1)
                    quantise("k", j - 1)
                elif what == "1":
                    for r in TILES:
                        transposes(nm1, j, r)
                        if j == 0 and r == MIDVAL:
                            values(0)
                elif what == "s" and j >= 1:
                    for r in range(R):
                        scores(j - 1, r)
                elif what == "o" and 2 <= j < LAST:
                    output(j - 2, 0, 2)
                    output(j - 2, 2, 2)
                    store(j - 2, 0, R)
            for b in VALUES_AT.get(j, ()):
                values(b)
            if 0 < j < LAST:
                pool_products(first_of(j + 1), j + 1, G_FIRST)
                pool_products(second_of(j + 1), j + 1, G_SECOND)
            for unit in range(3):
                products(nm2, j, unit, G_SECOND)

        quantise("k", LAST)
        transposes("q", LAST, 0, SC)
        transposes("q", LAST, 1, SC)
        quantise("s", LAST - 1)
        quantise("q", LAST, 0, 2)
        transposes("q", LAST, 3, VE)
        transposes("q", LAST, 2, SC)
        scores(LAST, 0, SC)
        scores(LAST, 1, VE)
        output(LAST - 2, 0, 2, SC)
        quantise("q", LAST, 2, 2)
        output(LAST - 2, 2, 2, VE)
        store(LAST - 2, 0, R)
        output(LAST - 1, 0, 2, SC)
        store(LAST - 1, 0, 2)
        scores(LAST, 2, SC)
        quantise("s", LAST, 0, 2)
        scores(LAST, 3, VE)
        output(LAST, 0, 2, SC)
        store(LAST, 0, 2)
        quantise("s", LAST, 2, 2)
        output(LAST - 1, 2, 2, VE)
        store(LAST - 1, 2, 2)
        output(LAST, 2, 1, SC)
        store(LAST, 2, 1)
        output(LAST, 3, 1, VE)
        store(LAST, 3, 1)
